import numpy as np
import ml_dtypes


def mxq(x, axis, fmt="e4m3"):
    dtype, down = {"e4m3": (ml_dtypes.float8_e4m3fn, 7), "e5m2": (ml_dtypes.float8_e5m2, 14)}[fmt]
    v = np.moveaxis(np.asarray(x, np.float32).astype(ml_dtypes.bfloat16).astype(np.float64), axis, -1)
    blocks = v.reshape(v.shape[:-1] + (-1, 32))
    amax = np.abs(blocks).max(-1, keepdims=True)
    byte = np.maximum(np.where(amax > 0, np.frexp(amax)[1] - 1 + 127, 0) - down, 1)
    scale = np.exp2(byte - 127.0)
    codes = (blocks / scale).astype(np.float32).astype(dtype).astype(np.float64)
    return np.moveaxis((codes * scale).reshape(v.shape), -1, axis)


WIDE = False


def mx_kscale(k):
    if not WIDE:
        return np.ones(k)
    levels = np.array([10, -10, 5, -5, 0])
    a = np.random.permutation(np.resize(levels, k // 512 * 4)).reshape(k // 512, 4)
    idx = np.arange(k)
    return np.exp2(a[idx // 512, idx % 128 // 32])


BF16 = ml_dtypes.bfloat16


def bf(x):
    return np.asarray(x, np.float32).astype(BF16)


def f64(x):
    return np.asarray(x).astype(np.float64)


E2M1 = np.array([0.0, 0.5, 1.0, 1.5, 2.0, 3.0, 4.0, 6.0, -0.0, -0.5, -1.0, -1.5, -2.0, -3.0, -4.0, -6.0])


def pack_weight(w, fmt):
    k, n = w.shape
    w = f64(bf(w)).reshape(k // 32, 32, n)
    amax = np.abs(w).max(1)
    if fmt == "e4m3":
        byte = np.frexp(amax)[1] - 1 + 127 - 7
    else:
        mant, ex = np.frexp(amax / 6.0)
        byte = np.where(mant > 0.5, ex, ex - 1) + 127
    byte = np.clip(np.where(amax > 0, byte, 1), 1, 254)
    scaled = (w * np.exp2(127.0 - byte)[:, None, :]).reshape(k, n).astype(np.float32)
    by_word = np.ascontiguousarray(scaled.reshape(k // 512, 128, 4, n).transpose(0, 1, 3, 2))
    if fmt == "e4m3":
        words = by_word.astype(ml_dtypes.float8_e4m3fn).view(np.uint8)
    else:
        c = by_word.astype(ml_dtypes.float4_e2m1fn).view(np.uint8) & 0xF
        words = c[..., 0::2] | (c[..., 1::2] << 4)
    return np.ascontiguousarray(words), np.ascontiguousarray(byte.astype(np.uint8).reshape(k // 512, 16, n))


def unpack_weight(words, scales, fmt):
    g, p, n, _ = words.shape
    if fmt == "e4m3":
        vals = np.ascontiguousarray(words).view(ml_dtypes.float8_e4m3fn).astype(np.float64)
    else:
        nib = np.empty((g, p, n, 4), np.uint8)
        nib[..., 0::2] = words & 0xF
        nib[..., 1::2] = words >> 4
        vals = E2M1[nib]
    vals = vals * np.repeat(np.exp2(scales.astype(np.float64) - 127.0), 8, axis=1)[..., None]
    return vals.transpose(0, 1, 3, 2).reshape(g * 512, n)


B, N, D, HEAD, HALF = 1, 1024, 512, 1024, 512
E = HEAD + HALF + HALF
EPS_RMS = 1e-6
EPS_NORM = 1e-12
FMT = "e4m3"


def setup_inputs():
    s = mx_kscale(D)
    x = bf(np.random.standard_normal((B, N, D)))
    g = bf((1.0 + 0.1 * np.random.standard_normal(D)) * s)
    words, scales = pack_weight(np.random.standard_normal((D, E)) / np.sqrt(D) / s[:, None], FMT)
    b1 = bf(np.random.standard_normal(E) * 0.3)
    return {"x": x,
            "g": g,
            "W1_words": words,
            "W1_scales": scales,
            "b1": b1}


def reference(x, g, W1_words, W1_scales, b1):
    x = f64(x)
    xn = x * (1.0 / np.sqrt(np.mean(np.square(x), axis=-1, keepdims=True) + EPS_RMS)) * f64(g)
    pre = (mxq(xn, 2, "e4m3") @ unpack_weight(W1_words, W1_scales, FMT)) + f64(b1)
    enriched = np.square(np.maximum(pre, 0.0))
    head = enriched[..., :HEAD]
    x_left = enriched[..., HEAD:HEAD + HALF]
    x_right = enriched[..., HEAD + HALF:]
    nrm = np.sqrt(np.sum(np.square(x_right), axis=-1, keepdims=True))
    xr_n = x_right / np.maximum(nrm, EPS_NORM)
    return head, x_left, xr_n

@@ -1,0 +1,179 @@
+from contextlib import ExitStack
+
+import concourse.mybir as mybir
+from concourse.masks import make_identity
+
+F32 = mybir.dt.float32
+BF16 = mybir.dt.bfloat16
+I32 = mybir.dt.int32
+U32 = mybir.dt.uint32
+U8 = mybir.dt.uint8
+FP8X4 = mybir.dt.float8_e4m3fn_x4
+ACT = mybir.ActivationFunctionType
+ALU = mybir.AluOpType
+
+P = 128
+PACK = 4
+TOKENS = 1024
+K = P * PACK
+HEAD = 1024
+HALF = 512
+FEATURES = HEAD + 2 * HALF
+BANK = 512
+N_TILES = TOKENS // P
+EPS_RMS = 1e-6
+EPS_NORM = 1e-12
+FLT_BIG = 3.0e38
+LEAD = 2
+
+FLOPS = 2 * TOKENS * K * FEATURES
+
+RIGHT = slice(HEAD + HALF, FEATURES)
+LEFT = slice(HEAD, HEAD + HALF)
+REST = slice(0, HEAD + HALF)
+BANKS_IN_ORDER = (3, 2, 0, 1)
+
+
+def tile_avey_pa_kernel(tc, x, g, W1_words, W1_scales, b1, out_0, out_1, out_2):
+    nc = tc.nc
+
+    x_rows = x.flatten_outer_dims().rearrange("(p i) k -> p i k", i=N_TILES)
+    head_rows = out_0.flatten_outer_dims().rearrange("(p i) n -> p i n", i=N_TILES)
+    left_rows = out_1.flatten_outer_dims().rearrange("(p i) n -> p i n", i=N_TILES)
+    right_rows = out_2.flatten_outer_dims().rearrange("(p i) n -> p i n", i=N_TILES)
+    w_bytes = W1_words.rearrange("o p n t -> p (o n t)")
+    w_scale_rows = W1_scales.rearrange("o q n -> (o q) n")
+
+    with ExitStack() as stack:
+        keep = stack.enter_context(tc.tile_pool(name="keep", bufs=1))
+        work = stack.enter_context(tc.tile_pool(name="work", bufs=3))
+        results = stack.enter_context(tc.tile_pool(name="results", bufs=4))
+        flip_banks = stack.enter_context(tc.psum_pool(name="flip_banks", bufs=2))
+        acc_banks = stack.enter_context(tc.psum_pool(name="acc_banks", bufs=6))
+
+        x_sb = keep.tile([P, N_TILES, K], BF16)
+        gain = keep.tile([P, PACK], BF16)
+        bias = keep.tile([P, FEATURES], BF16)
+        w_codes = keep.tile([P, FEATURES], U32, align_bytes=64)
+        w_scales = keep.tile([P, FEATURES], U8, align_bytes=64)
+        xq_codes = keep.tile([P, N_TILES, P], U32, align_bytes=64)
+        xq_scales = keep.tile([P, N_TILES, P], U8, align_bytes=64)
+        identity = keep.tile([P, P], F32)
+        eps_rms = keep.tile([P, 1], F32)
+        table_warm = keep.tile([P, 1], F32)
+        sum_sq = keep.tile([P, N_TILES], F32)
+        rms = keep.tile([P, N_TILES], F32)
+        rstd = keep.tile([P, N_TILES], F32)
+        right_sq = keep.tile([P, N_TILES], F32)
+        right_norm = keep.tile([P, N_TILES], F32)
+        right_floor = keep.tile([P, N_TILES], F32)
+        right_inv = keep.tile([P, N_TILES], F32)
+
+        nc.vector.memset(w_scales[:].bitcast(I32), 0)
+        nc.vector.memset(eps_rms[:], EPS_RMS)
+        nc.scalar.activation(out=table_warm[:], in_=eps_rms[:], func=ACT.Sqrt)
+        make_identity(nc, identity[:])
+
+        nc.scalar.dma_start(out=bias[:], in_=b1.partition_broadcast(P))
+        nc.sync.dma_start(out=x_sb[:, 0:1, :], in_=x_rows[:, 0:1, :])
+        nc.sync.dma_start(out=gain[:], in_=g.rearrange("(p t) -> p t", t=PACK))
+        for quadrant in range(4):
+            nc.sync.dma_start(
+                out=w_scales[32 * quadrant : 32 * quadrant + 4, :].bitcast(I32),
+                in_=w_scale_rows[4 * quadrant : 4 * quadrant + 4, :].bitcast(I32),
+            )
+        nc.sync.dma_start(out=x_sb[:, 1:2, :], in_=x_rows[:, 1:2, :])
+        nc.sync.dma_start(
+            out=w_codes[:, HEAD:FEATURES].bitcast(I32),
+            in_=w_bytes[:, PACK * HEAD : PACK * FEATURES].bitcast(I32),
+        )
+        nc.sync.dma_start(out=x_sb[:, 2:4, :], in_=x_rows[:, 2:4, :])
+        nc.sync.dma_start(
+            out=w_codes[:, 0:HEAD].bitcast(I32), in_=w_bytes[:, 0 : PACK * HEAD].bitcast(I32)
+        )
+        nc.sync.dma_start(out=x_sb[:, 4:N_TILES, :], in_=x_rows[:, 4:N_TILES, :])
+
+        def normalise_and_quantise(i):
+            col = slice(i, i + 1)
+            squares = work.tile([P, K], BF16)
+            nc.scalar.activation(
+                out=squares[:], in_=x_sb[:, i, :], func=ACT.Square, accum_out=sum_sq[:, col]
+            )
+            nc.scalar.activation(
+                out=rms[:, col], in_=sum_sq[:, col], func=ACT.Sqrt, scale=1.0 / K, bias=eps_rms[:]
+            )
+            nc.vector.reciprocal(out=rstd[:, col], in_=rms[:, col])
+            scaled = work.tile([P, PACK, P], F32)
+            nc.gpsimd.tensor_scalar(
+                out=scaled[:],
+                in0=x_sb[:, i, :].rearrange("p (q t) -> p t q", t=PACK),
+                scalar1=rstd[:, col],
+                scalar2=1.0,
+                op0=ALU.mult,
+                op1=ALU.mult,
+            )
+            flipped = flip_banks.tile([P, PACK, P], F32)
+            for t in range(PACK):
+                nc.tensor.transpose(flipped[:, t, :], scaled[:, t, :], identity[:])
+            grouped = work.tile([P, P, PACK], BF16, align_bytes=64)
+            nc.vector.tensor_tensor(
+                out=grouped[:],
+                in0=flipped[:].rearrange("q t r -> q r t"),
+                in1=gain[:].unsqueeze(1).to_broadcast([P, P, PACK]),
+                op=ALU.mult,
+            )
+            nc.vector.quantize_mx(
+                out=xq_codes[:, i, :].bitcast(FP8X4),
+                scales=xq_scales[:, i, :],
+                in_=grouped[:].rearrange("q r t -> q (r t)"),
+            )
+
+        def project_and_store(i):
+            col = slice(i, i + 1)
+            enriched = results.tile([P, FEATURES], F32)
+            for bank in BANKS_IN_ORDER:
+                cols = slice(bank * BANK, (bank + 1) * BANK)
+                acc = acc_banks.tile([P, BANK], F32)
+                nc.tensor.matmul_mx(
+                    out=acc[:],
+                    lhsT=xq_codes[:, i, :].bitcast(FP8X4),
+                    lhsT_scale=xq_scales[:, i, :],
+                    rhs=w_codes[:, cols].bitcast(FP8X4),
+                    rhs_scale=w_scales[:, cols],
+                    start=True,
+                    stop=True,
+                )
+                nc.vector.tensor_tensor(
+                    out=enriched[:, cols], in0=acc[:], in1=bias[:, cols], op=ALU.add
+                )
+            for part in (RIGHT, REST):
+                nc.gpsimd.tensor_scalar(
+                    out=enriched[:, part],
+                    in0=enriched[:, part],
+                    scalar1=FLT_BIG,
+                    scalar2=0.0,
+                    op0=ALU.min,
+                    op1=ALU.max,
+                )
+                nc.scalar.activation(out=enriched[:, part], in_=enriched[:, part], func=ACT.Square)
+            fourth = work.tile([P, HALF], F32)
+            nc.scalar.activation(
+                out=fourth[:], in_=enriched[:, RIGHT], func=ACT.Square, accum_out=right_sq[:, col]
+            )
+            nc.scalar.activation(out=right_norm[:, col], in_=right_sq[:, col], func=ACT.Sqrt)
+            nc.vector.tensor_scalar_max(
+                out=right_floor[:, col], in0=right_norm[:, col], scalar1=EPS_NORM
+            )
+            nc.vector.reciprocal(out=right_inv[:, col], in_=right_floor[:, col])
+            nc.vector.tensor_scalar_mul(
+                out=enriched[:, RIGHT], in0=enriched[:, RIGHT], scalar1=right_inv[:, col]
+            )
+            nc.sync.dma_start(out=head_rows[:, i, :], in_=enriched[:, 0:HEAD])
+            nc.sync.dma_start(out=left_rows[:, i, :], in_=enriched[:, LEFT])
+            nc.sync.dma_start(out=right_rows[:, i, :], in_=enriched[:, RIGHT])
+
+        for step in range(N_TILES + LEAD):
+            if step < N_TILES:
+                normalise_and_quantise(step)
+            if step >= LEAD:
+                project_and_store(step - LEAD)

@@ -24,27 +24,32 @@ N_TILES = TOKENS // P
 EPS_RMS = 1e-6
 EPS_NORM = 1e-12
 FLT_BIG = 3.0e38
-LEAD = 2
+QUANTISE_AHEAD = 2
+SCALE_AHEAD = 4
 
 FLOPS = 2 * TOKENS * K * FEATURES
 
-RIGHT = slice(HEAD + HALF, FEATURES)
-LEFT = slice(HEAD, HEAD + HALF)
-REST = slice(0, HEAD + HALF)
-BANKS_IN_ORDER = (3, 2, 0, 1)
+X_PIECES = ((0, 1), (1, 2), (2, 4), (4, 8))
+RIGHT = (HEAD + HALF, FEATURES)
+HEAD_PART = (0, HEAD)
+LEFT = (HEAD, HEAD + HALF)
+PARTS = (RIGHT, HEAD_PART, LEFT)
 
 
 def tile_avey_pa_kernel(tc, x, g, W1_words, W1_scales, b1, out_0, out_1, out_2):
     nc = tc.nc
 
     x_rows = x.flatten_outer_dims().rearrange("(p i) k -> p i k", i=N_TILES)
-    head_rows = out_0.flatten_outer_dims().rearrange("(p i) n -> p i n", i=N_TILES)
-    left_rows = out_1.flatten_outer_dims().rearrange("(p i) n -> p i n", i=N_TILES)
-    right_rows = out_2.flatten_outer_dims().rearrange("(p i) n -> p i n", i=N_TILES)
+    out_rows = {
+        RIGHT: out_2.flatten_outer_dims().rearrange("(p i) n -> p i n", i=N_TILES),
+        HEAD_PART: out_0.flatten_outer_dims().rearrange("(p i) n -> p i n", i=N_TILES),
+        LEFT: out_1.flatten_outer_dims().rearrange("(p i) n -> p i n", i=N_TILES),
+    }
     w_bytes = W1_words.rearrange("o p n t -> p (o n t)")
     w_scale_rows = W1_scales.rearrange("o q n -> (o q) n")
 
     with ExitStack() as stack:
+        stack.enter_context(tc.manual_schedule())
         keep = stack.enter_context(tc.tile_pool(name="keep", bufs=1))
         work = stack.enter_context(tc.tile_pool(name="work", bufs=3))
         results = stack.enter_context(tc.tile_pool(name="results", bufs=4))
@@ -52,6 +57,7 @@ def tile_avey_pa_kernel(tc, x, g, W1_words, W1_scales, b1, out_0, out_1, out_2):
         acc_banks = stack.enter_context(tc.psum_pool(name="acc_banks", bufs=6))
 
         x_sb = keep.tile([P, N_TILES, K], BF16)
+        scaled = keep.tile([P, N_TILES, PACK, P], F32)
         gain = keep.tile([P, PACK], BF16)
         bias = keep.tile([P, FEATURES], BF16)
         w_codes = keep.tile([P, FEATURES], U32, align_bytes=64)
@@ -62,59 +68,74 @@ def tile_avey_pa_kernel(tc, x, g, W1_words, W1_scales, b1, out_0, out_1, out_2):
         eps_rms = keep.tile([P, 1], F32)
         table_warm = keep.tile([P, 1], F32)
         sum_sq = keep.tile([P, N_TILES], F32)
-        rms = keep.tile([P, N_TILES], F32)
         rstd = keep.tile([P, N_TILES], F32)
         right_sq = keep.tile([P, N_TILES], F32)
-        right_norm = keep.tile([P, N_TILES], F32)
-        right_floor = keep.tile([P, N_TILES], F32)
+        right_rsqrt = keep.tile([P, N_TILES], F32)
         right_inv = keep.tile([P, N_TILES], F32)
 
         nc.vector.memset(w_scales[:].bitcast(I32), 0)
         nc.vector.memset(eps_rms[:], EPS_RMS)
-        nc.scalar.activation(out=table_warm[:], in_=eps_rms[:], func=ACT.Sqrt)
+        nc.scalar.activation(out=table_warm[:], in_=eps_rms[:], func=ACT.Abs_reciprocal_sqrt)
         make_identity(nc, identity[:])
 
+        def load_x(piece):
+            first, end = piece
+            nc.sync.dma_start(out=x_sb[:, first:end, :], in_=x_rows[:, first:end, :])
+
+        def load_w(part):
+            first, end = part
+            nc.sync.dma_start(
+                out=w_codes[:, first:end].bitcast(I32),
+                in_=w_bytes[:, PACK * first : PACK * end].bitcast(I32),
+            )
+
         nc.scalar.dma_start(out=bias[:], in_=b1.partition_broadcast(P))
-        nc.sync.dma_start(out=x_sb[:, 0:1, :], in_=x_rows[:, 0:1, :])
-        nc.sync.dma_start(out=gain[:], in_=g.rearrange("(p t) -> p t", t=PACK))
+        load_x(X_PIECES[0])
+        nc.sync.dma_start(out=gain[:], in_=g.rearrange("(q t) -> q t", t=PACK))
         for quadrant in range(4):
             nc.sync.dma_start(
                 out=w_scales[32 * quadrant : 32 * quadrant + 4, :].bitcast(I32),
                 in_=w_scale_rows[4 * quadrant : 4 * quadrant + 4, :].bitcast(I32),
             )
-        nc.sync.dma_start(out=x_sb[:, 1:2, :], in_=x_rows[:, 1:2, :])
-        nc.sync.dma_start(
-            out=w_codes[:, HEAD:FEATURES].bitcast(I32),
-            in_=w_bytes[:, PACK * HEAD : PACK * FEATURES].bitcast(I32),
-        )
-        nc.sync.dma_start(out=x_sb[:, 2:4, :], in_=x_rows[:, 2:4, :])
-        nc.sync.dma_start(
-            out=w_codes[:, 0:HEAD].bitcast(I32), in_=w_bytes[:, 0 : PACK * HEAD].bitcast(I32)
-        )
-        nc.sync.dma_start(out=x_sb[:, 4:N_TILES, :], in_=x_rows[:, 4:N_TILES, :])
+        load_x(X_PIECES[1])
+        load_w(RIGHT)
+        load_x(X_PIECES[2])
+        load_w(HEAD_PART)
+        load_w(LEFT)
+        load_x(X_PIECES[3])
 
-        def normalise_and_quantise(i):
-            col = slice(i, i + 1)
-            squares = work.tile([P, K], BF16)
+        def reciprocal_rms(piece):
+            first, end = piece
+            for i in range(first, end):
+                squares = work.tile([P, K], BF16)
+                nc.scalar.activation(
+                    out=squares[:],
+                    in_=x_sb[:, i, :],
+                    func=ACT.Square,
+                    accum_out=sum_sq[:, i : i + 1],
+                )
             nc.scalar.activation(
-                out=squares[:], in_=x_sb[:, i, :], func=ACT.Square, accum_out=sum_sq[:, col]
+                out=rstd[:, first:end],
+                in_=sum_sq[:, first:end],
+                func=ACT.Abs_reciprocal_sqrt,
+                scale=1.0 / K,
+                bias=eps_rms[:],
             )
-            nc.scalar.activation(
-                out=rms[:, col], in_=sum_sq[:, col], func=ACT.Sqrt, scale=1.0 / K, bias=eps_rms[:]
-            )
-            nc.vector.reciprocal(out=rstd[:, col], in_=rms[:, col])
-            scaled = work.tile([P, PACK, P], F32)
+
+        def scale_rows(i):
             nc.gpsimd.tensor_scalar(
-                out=scaled[:],
+                out=scaled[:, i, :, :],
                 in0=x_sb[:, i, :].rearrange("p (q t) -> p t q", t=PACK),
-                scalar1=rstd[:, col],
+                scalar1=rstd[:, i : i + 1],
                 scalar2=1.0,
                 op0=ALU.mult,
                 op1=ALU.mult,
             )
+
+        def flip_and_quantise(i):
             flipped = flip_banks.tile([P, PACK, P], F32)
             for t in range(PACK):
-                nc.tensor.transpose(flipped[:, t, :], scaled[:, t, :], identity[:])
+                nc.tensor.transpose(flipped[:, t, :], scaled[:, i, t, :], identity[:])
             grouped = work.tile([P, P, PACK], BF16, align_bytes=64)
             nc.vector.tensor_tensor(
                 out=grouped[:],
@@ -128,52 +149,77 @@ def tile_avey_pa_kernel(tc, x, g, W1_words, W1_scales, b1, out_0, out_1, out_2):
                 in_=grouped[:].rearrange("q r t -> q (r t)"),
             )
 
-        def project_and_store(i):
-            col = slice(i, i + 1)
-            enriched = results.tile([P, FEATURES], F32)
-            for bank in BANKS_IN_ORDER:
-                cols = slice(bank * BANK, (bank + 1) * BANK)
-                acc = acc_banks.tile([P, BANK], F32)
-                nc.tensor.matmul_mx(
-                    out=acc[:],
-                    lhsT=xq_codes[:, i, :].bitcast(FP8X4),
-                    lhsT_scale=xq_scales[:, i, :],
-                    rhs=w_codes[:, cols].bitcast(FP8X4),
-                    rhs_scale=w_scales[:, cols],
-                    start=True,
-                    stop=True,
-                )
-                nc.vector.tensor_tensor(
-                    out=enriched[:, cols], in0=acc[:], in1=bias[:, cols], op=ALU.add
-                )
-            for part in (RIGHT, REST):
-                nc.gpsimd.tensor_scalar(
-                    out=enriched[:, part],
-                    in0=enriched[:, part],
-                    scalar1=FLT_BIG,
-                    scalar2=0.0,
-                    op0=ALU.min,
-                    op1=ALU.max,
-                )
-                nc.scalar.activation(out=enriched[:, part], in_=enriched[:, part], func=ACT.Square)
+        def product_plus_bias(i):
+            pre = {}
+            for part in PARTS:
+                first, end = part
+                pre[part] = results.tile([P, end - first], F32, name="pre_%d" % first)
+                for start in range(first, end, BANK):
+                    cols = slice(start, start + BANK)
+                    acc = acc_banks.tile([P, BANK], F32)
+                    nc.tensor.matmul_mx(
+                        out=acc[:],
+                        lhsT=xq_codes[:, i, :].bitcast(FP8X4),
+                        lhsT_scale=xq_scales[:, i, :],
+                        rhs=w_codes[:, cols].bitcast(FP8X4),
+                        rhs_scale=w_scales[:, cols],
+                        start=True,
+                        stop=True,
+                    )
+                    nc.vector.tensor_tensor(
+                        out=pre[part][:, start - first : start - first + BANK],
+                        in0=acc[:],
+                        in1=bias[:, cols],
+                        op=ALU.add,
+                    )
+            return pre
+
+        def squared_relu(tile):
+            nc.gpsimd.tensor_scalar(
+                out=tile[:], in0=tile[:], scalar1=FLT_BIG, scalar2=0.0, op0=ALU.min, op1=ALU.max
+            )
+            nc.scalar.activation(out=tile[:], in_=tile[:], func=ACT.Square)
+
+        def right_norm(i, right):
             fourth = work.tile([P, HALF], F32)
             nc.scalar.activation(
-                out=fourth[:], in_=enriched[:, RIGHT], func=ACT.Square, accum_out=right_sq[:, col]
+                out=fourth[:], in_=right[:], func=ACT.Square, accum_out=right_sq[:, i : i + 1]
             )
-            nc.scalar.activation(out=right_norm[:, col], in_=right_sq[:, col], func=ACT.Sqrt)
-            nc.vector.tensor_scalar_max(
-                out=right_floor[:, col], in0=right_norm[:, col], scalar1=EPS_NORM
+            nc.scalar.activation(
+                out=right_rsqrt[:, i : i + 1],
+                in_=right_sq[:, i : i + 1],
+                func=ACT.Abs_reciprocal_sqrt,
             )
-            nc.vector.reciprocal(out=right_inv[:, col], in_=right_floor[:, col])
-            nc.vector.tensor_scalar_mul(
-                out=enriched[:, RIGHT], in0=enriched[:, RIGHT], scalar1=right_inv[:, col]
-            )
-            nc.sync.dma_start(out=head_rows[:, i, :], in_=enriched[:, 0:HEAD])
-            nc.sync.dma_start(out=left_rows[:, i, :], in_=enriched[:, LEFT])
-            nc.sync.dma_start(out=right_rows[:, i, :], in_=enriched[:, RIGHT])
 
-        for step in range(N_TILES + LEAD):
-            if step < N_TILES:
-                normalise_and_quantise(step)
-            if step >= LEAD:
-                project_and_store(step - LEAD)
+        def store(i, part, tile):
+            nc.sync.dma_start(out=out_rows[part][:, i, :], in_=tile[:])
+
+        def normalise_right(i, right):
+            nc.vector.tensor_scalar_min(
+                out=right_inv[:, i : i + 1], in0=right_rsqrt[:, i : i + 1], scalar1=1.0 / EPS_NORM
+            )
+            nc.vector.tensor_scalar_mul(out=right[:], in0=right[:], scalar1=right_inv[:, i : i + 1])
+            store(i, RIGHT, right)
+
+        for piece in X_PIECES:
+            reciprocal_rms(piece)
+        for i in range(SCALE_AHEAD):
+            scale_rows(i)
+        for i in range(QUANTISE_AHEAD):
+            flip_and_quantise(i)
+        rights = {}
+        for i in range(N_TILES):
+            pre = product_plus_bias(i)
+            rights[i] = pre[RIGHT]
+            if i + QUANTISE_AHEAD < N_TILES:
+                flip_and_quantise(i + QUANTISE_AHEAD)
+            if i > 0:
+                normalise_right(i - 1, rights[i - 1])
+            squared_relu(pre[RIGHT])
+            right_norm(i, pre[RIGHT])
+            for part in (HEAD_PART, LEFT):
+                squared_relu(pre[part])
+                store(i, part, pre[part])
+            if i + SCALE_AHEAD < N_TILES:
+                scale_rows(i + SCALE_AHEAD)
+        normalise_right(N_TILES - 1, rights[N_TILES - 1])

@@ -24,8 +24,6 @@ N_TILES = TOKENS // P
 EPS_RMS = 1e-6
 EPS_NORM = 1e-12
 FLT_BIG = 3.0e38
-QUANTISE_AHEAD = 2
-SCALE_AHEAD = 4
 
 FLOPS = 2 * TOKENS * K * FEATURES
 
@@ -52,12 +50,13 @@ def tile_avey_pa_kernel(tc, x, g, W1_words, W1_scales, b1, out_0, out_1, out_2):
         stack.enter_context(tc.manual_schedule())
         keep = stack.enter_context(tc.tile_pool(name="keep", bufs=1))
         work = stack.enter_context(tc.tile_pool(name="work", bufs=3))
-        results = stack.enter_context(tc.tile_pool(name="results", bufs=4))
+        results = stack.enter_context(tc.tile_pool(name="results", bufs=N_TILES))
         flip_banks = stack.enter_context(tc.psum_pool(name="flip_banks", bufs=2))
         acc_banks = stack.enter_context(tc.psum_pool(name="acc_banks", bufs=6))
 
         x_sb = keep.tile([P, N_TILES, K], BF16)
         scaled = keep.tile([P, N_TILES, PACK, P], F32)
+        grouped = keep.tile([P, N_TILES, P, PACK], BF16, align_bytes=64)
         gain = keep.tile([P, PACK], BF16)
         bias = keep.tile([P, FEATURES], BF16)
         w_codes = keep.tile([P, FEATURES], U32, align_bytes=64)
@@ -72,9 +71,14 @@ def tile_avey_pa_kernel(tc, x, g, W1_words, W1_scales, b1, out_0, out_1, out_2):
         right_sq = keep.tile([P, N_TILES], F32)
         right_rsqrt = keep.tile([P, N_TILES], F32)
         right_inv = keep.tile([P, N_TILES], F32)
+        unused_sum = keep.tile([P, N_TILES], F32)
+        floor = keep.tile([P, 1], F32)
+        neg_floor = keep.tile([P, 1], F32)
 
         nc.vector.memset(w_scales[:].bitcast(I32), 0)
         nc.vector.memset(eps_rms[:], EPS_RMS)
+        nc.vector.memset(floor[:], EPS_NORM * EPS_NORM)
+        nc.vector.memset(neg_floor[:], -EPS_NORM * EPS_NORM)
         nc.scalar.activation(out=table_warm[:], in_=eps_rms[:], func=ACT.Abs_reciprocal_sqrt)
         make_identity(nc, identity[:])
 
@@ -104,16 +108,13 @@ def tile_avey_pa_kernel(tc, x, g, W1_words, W1_scales, b1, out_0, out_1, out_2):
         load_w(LEFT)
         load_x(X_PIECES[3])
 
-        def reciprocal_rms(piece):
-            first, end = piece
-            for i in range(first, end):
-                squares = work.tile([P, K], BF16)
-                nc.scalar.activation(
-                    out=squares[:],
-                    in_=x_sb[:, i, :],
-                    func=ACT.Square,
-                    accum_out=sum_sq[:, i : i + 1],
-                )
+        def mean_square(i):
+            squares = work.tile([P, K], BF16)
+            nc.scalar.activation(
+                out=squares[:], in_=x_sb[:, i, :], func=ACT.Square, accum_out=sum_sq[:, i : i + 1]
+            )
+
+        def reciprocal_rms(first, end):
             nc.scalar.activation(
                 out=rstd[:, first:end],
                 in_=sum_sq[:, first:end],
@@ -122,104 +123,246 @@ def tile_avey_pa_kernel(tc, x, g, W1_words, W1_scales, b1, out_0, out_1, out_2):
                 bias=eps_rms[:],
             )
 
-        def scale_rows(i):
-            nc.gpsimd.tensor_scalar(
+        def scale_rows_vector(i):
+            nc.vector.tensor_scalar_mul(
                 out=scaled[:, i, :, :],
                 in0=x_sb[:, i, :].rearrange("p (q t) -> p t q", t=PACK),
                 scalar1=rstd[:, i : i + 1],
-                scalar2=1.0,
-                op0=ALU.mult,
-                op1=ALU.mult,
             )
 
-        def flip_and_quantise(i):
-            flipped = flip_banks.tile([P, PACK, P], F32)
+        def scale_rows_one_port(i):
+            nc.vector.tensor_scalar(
+                out=scaled[:, i, :, :],
+                in0=x_sb[:, i, :].rearrange("p (q t) -> p t q", t=PACK),
+                scalar1=rstd[:, i : i + 1],
+                scalar2=None,
+                op0=ALU.mult,
+                op1=ALU.add,
+                accum_out=unused_sum[:, i : i + 1],
+            )
+
+        def scale_rows_scalar(i):
+            nc.scalar.activation(
+                out=scaled[:, i, :, :],
+                in_=x_sb[:, i, :].rearrange("p (q t) -> p t q", t=PACK),
+                func=ACT.Copy,
+                scale=rstd[:, i : i + 1],
+            )
+
+        flipped = {}
+
+        def flip(i):
+            flipped[i] = flip_banks.tile([P, PACK, P], F32, name="flipped")
             for t in range(PACK):
-                nc.tensor.transpose(flipped[:, t, :], scaled[:, i, t, :], identity[:])
-            grouped = work.tile([P, P, PACK], BF16, align_bytes=64)
+                nc.tensor.transpose(flipped[i][:, t, :], scaled[:, i, t, :], identity[:])
+
+        def apply_gain(i):
             nc.vector.tensor_tensor(
-                out=grouped[:],
-                in0=flipped[:].rearrange("q t r -> q r t"),
+                out=grouped[:, i, :, :],
+                in0=flipped[i][:].rearrange("q t r -> q r t"),
                 in1=gain[:].unsqueeze(1).to_broadcast([P, P, PACK]),
                 op=ALU.mult,
             )
+
+        def quantise(i):
             nc.vector.quantize_mx(
                 out=xq_codes[:, i, :].bitcast(FP8X4),
                 scales=xq_scales[:, i, :],
-                in_=grouped[:].rearrange("q r t -> q (r t)"),
+                in_=grouped[:, i, :, :].rearrange("q r t -> q (r t)"),
             )
 
-        def product_plus_bias(i):
-            pre = {}
-            for part in PARTS:
-                first, end = part
-                pre[part] = results.tile([P, end - first], F32, name="pre_%d" % first)
-                for start in range(first, end, BANK):
-                    cols = slice(start, start + BANK)
-                    acc = acc_banks.tile([P, BANK], F32)
-                    nc.tensor.matmul_mx(
-                        out=acc[:],
-                        lhsT=xq_codes[:, i, :].bitcast(FP8X4),
-                        lhsT_scale=xq_scales[:, i, :],
-                        rhs=w_codes[:, cols].bitcast(FP8X4),
-                        rhs_scale=w_scales[:, cols],
-                        start=True,
-                        stop=True,
-                    )
-                    nc.vector.tensor_tensor(
-                        out=pre[part][:, start - first : start - first + BANK],
-                        in0=acc[:],
-                        in1=bias[:, cols],
-                        op=ALU.add,
-                    )
-            return pre
+        pre = {}
+        accs = {}
 
-        def squared_relu(tile):
+        def product(i, start):
+            cols = slice(start, start + BANK)
+            accs[(i, start)] = acc_banks.tile([P, BANK], F32, name="acc")
+            nc.tensor.matmul_mx(
+                out=accs[(i, start)][:],
+                lhsT=xq_codes[:, i, :].bitcast(FP8X4),
+                lhsT_scale=xq_scales[:, i, :],
+                rhs=w_codes[:, cols].bitcast(FP8X4),
+                rhs_scale=w_scales[:, cols],
+                start=True,
+                stop=True,
+            )
+
+        def add_bias(i, part, start):
+            first = part[0]
+            nc.vector.tensor_tensor(
+                out=pre[(i, part)][:, start - first : start - first + BANK],
+                in0=accs[(i, start)][:],
+                in1=bias[:, start : start + BANK],
+                op=ALU.add,
+            )
+
+        def relu_pool(view):
             nc.gpsimd.tensor_scalar(
-                out=tile[:], in0=tile[:], scalar1=FLT_BIG, scalar2=0.0, op0=ALU.min, op1=ALU.max
+                out=view, in0=view, scalar1=FLT_BIG, scalar2=0.0, op0=ALU.min, op1=ALU.max
             )
-            nc.scalar.activation(out=tile[:], in_=tile[:], func=ACT.Square)
 
-        def right_norm(i, right):
+        def squared_relu_vector(view):
+            nc.vector.scalar_tensor_tensor(
+                out=view, in0=view, scalar=0.0, in1=view, op0=ALU.max, op1=ALU.mult
+            )
+
+        def square(view):
+            nc.scalar.activation(out=view, in_=view, func=ACT.Square)
+
+        def right_norm(i):
             fourth = work.tile([P, HALF], F32)
             nc.scalar.activation(
-                out=fourth[:], in_=right[:], func=ACT.Square, accum_out=right_sq[:, i : i + 1]
+                out=fourth[:], in_=pre[(i, RIGHT)][:], func=ACT.Square, accum_out=right_sq[:, i : i + 1]
             )
             nc.scalar.activation(
                 out=right_rsqrt[:, i : i + 1],
                 in_=right_sq[:, i : i + 1],
+                func=ACT.Relu,
+                bias=neg_floor[:],
+            )
+            nc.scalar.activation(
+                out=right_inv[:, i : i + 1],
+                in_=right_rsqrt[:, i : i + 1],
                 func=ACT.Abs_reciprocal_sqrt,
+                bias=floor[:],
             )
 
-        def store(i, part, tile):
-            nc.sync.dma_start(out=out_rows[part][:, i, :], in_=tile[:])
+        def store(i, part):
+            nc.sync.dma_start(out=out_rows[part][:, i, :], in_=pre[(i, part)][:])
 
-        def normalise_right(i, right):
-            nc.vector.tensor_scalar_min(
-                out=right_inv[:, i : i + 1], in0=right_rsqrt[:, i : i + 1], scalar1=1.0 / EPS_NORM
+        def normalise_right_pool(i):
+            nc.gpsimd.tensor_scalar(
+                out=pre[(i, RIGHT)][:],
+                in0=pre[(i, RIGHT)][:],
+                scalar1=right_inv[:, i : i + 1],
+                scalar2=1.0,
+                op0=ALU.mult,
+                op1=ALU.mult,
             )
-            nc.vector.tensor_scalar_mul(out=right[:], in0=right[:], scalar1=right_inv[:, i : i + 1])
-            store(i, RIGHT, right)
+            store(i, RIGHT)
 
-        for piece in X_PIECES:
-            reciprocal_rms(piece)
-        for i in range(SCALE_AHEAD):
-            scale_rows(i)
-        for i in range(QUANTISE_AHEAD):
-            flip_and_quantise(i)
-        rights = {}
+        def normalise_right_vector(i):
+            nc.vector.tensor_scalar_mul(
+                out=pre[(i, RIGHT)][:], in0=pre[(i, RIGHT)][:], scalar1=right_inv[:, i : i + 1]
+            )
+            store(i, RIGHT)
+
+        R0 = RIGHT[0]
+        L0 = LEFT[0]
+        WIDE = (0, HEAD + HALF)
+
+        def add_bias_wide(i, start):
+            nc.vector.tensor_tensor(
+                out=pre[(i, WIDE)][:, start : start + BANK],
+                in0=accs[(i, start)][:],
+                in1=bias[:, start : start + BANK],
+                op=ALU.add,
+            )
+
+        def store_head(i):
+            nc.sync.dma_start(out=out_rows[HEAD_PART][:, i, :], in_=pre[(i, WIDE)][:, 0:HEAD])
+
+        def store_left(i):
+            nc.sync.dma_start(out=out_rows[LEFT][:, i, :], in_=pre[(i, WIDE)][:, HEAD : HEAD + HALF])
+
+        def sum_fourth(i):
+            fourth = work.tile([P, HALF], F32)
+            nc.scalar.activation(
+                out=fourth[:], in_=pre[(i, RIGHT)][:], func=ACT.Square, accum_out=right_sq[:, i : i + 1]
+            )
+
+        def floor_sum(i):
+            nc.scalar.activation(
+                out=right_rsqrt[:, i : i + 1], in_=right_sq[:, i : i + 1], func=ACT.Relu, bias=neg_floor[:]
+            )
+
+        def inverse_norm(i):
+            nc.scalar.activation(
+                out=right_inv[:, i : i + 1],
+                in_=right_rsqrt[:, i : i + 1],
+                func=ACT.Abs_reciprocal_sqrt,
+                bias=floor[:],
+            )
+
+        mean_square(0)
+        reciprocal_rms(0, 1)
+        scale_rows_vector(0)
+        flip(0)
+        mean_square(1)
+        reciprocal_rms(1, 2)
+        scale_rows_vector(1)
+        flip(1)
+        apply_gain(0)
+        mean_square(2)
+        mean_square(3)
+        reciprocal_rms(2, 4)
+        scale_rows_vector(2)
+        quantise(0)
+        apply_gain(1)
+        scale_rows_scalar(3)
+
+        LAST = N_TILES - 1
         for i in range(N_TILES):
-            pre = product_plus_bias(i)
-            rights[i] = pre[RIGHT]
-            if i + QUANTISE_AHEAD < N_TILES:
-                flip_and_quantise(i + QUANTISE_AHEAD)
+            pre[(i, RIGHT)] = results.tile([P, HALF], F32, name="pre_right")
+            pre[(i, WIDE)] = results.tile([P, HEAD + HALF], F32, name="pre_wide")
+            wide = pre[(i, WIDE)]
+            before = pre.get((i - 1, WIDE))
+            product(i, R0)
+            add_bias(i, RIGHT, R0)
+            product(i, 0)
+            add_bias_wide(i, 0)
+            if i == LAST:
+                squared_relu_vector(pre[(i, RIGHT)][:])
+            product(i, BANK)
+            add_bias_wide(i, BANK)
+            product(i, L0)
+            add_bias_wide(i, L0)
+            if i + 1 < N_TILES:
+                quantise(i + 1)
+            if i + 2 < N_TILES:
+                flip(i + 2)
+                apply_gain(i + 2)
+            if 4 <= i + 3 < N_TILES:
+                scale_rows_one_port(i + 3)
+            if i < LAST:
+                relu_pool(pre[(i, RIGHT)][:])
             if i > 0:
-                normalise_right(i - 1, rights[i - 1])
-            squared_relu(pre[RIGHT])
-            right_norm(i, pre[RIGHT])
-            for part in (HEAD_PART, LEFT):
-                squared_relu(pre[part])
-                store(i, part, pre[part])
-            if i + SCALE_AHEAD < N_TILES:
-                scale_rows(i + SCALE_AHEAD)
-        normalise_right(N_TILES - 1, rights[N_TILES - 1])
+                normalise_right_pool(i - 1)
+            if i < LAST:
+                relu_pool(wide[:])
+            else:
+                relu_pool(wide[:, 0:BANK])
+            if i > 0:
+                square(before[:, 0:BANK])
+            if i < LAST:
+                square(pre[(i, RIGHT)][:])
+            else:
+                sum_fourth(i)
+            if i > 0:
+                square(before[:, BANK : 2 * BANK])
+                store_head(i - 1)
+            if i < LAST:
+                sum_fourth(i)
+            else:
+                floor_sum(i)
+            if i > 0:
+                square(before[:, HEAD : HEAD + HALF])
+                store_left(i - 1)
+            if i < LAST:
+                floor_sum(i)
+            if i == 0:
+                mean_square(4)
+                mean_square(5)
+                reciprocal_rms(4, 6)
+            if i == 1:
+                mean_square(6)
+                mean_square(7)
+                reciprocal_rms(6, 8)
+            inverse_norm(i)
+            if i == LAST:
+                squared_relu_vector(wide[:, BANK : 2 * BANK])
+                squared_relu_vector(wide[:, HEAD : HEAD + HALF])
+                store_left(i)
+                square(wide[:, 0:BANK])
+                store_head(i)
+                normalise_right_vector(i)

@@ -59,6 +59,8 @@ def tile_avey_pa_kernel(tc, x, g, W1_words, W1_scales, b1, out_0, out_1, out_2):
         grouped = keep.tile([P, N_TILES, P, PACK], BF16, align_bytes=64)
         gain = keep.tile([P, PACK], BF16)
         bias = keep.tile([P, FEATURES], BF16)
+        bias_row = keep.tile([P, FEATURES], BF16)
+        ones = keep.tile([P, P], BF16)
         w_codes = keep.tile([P, FEATURES], U32, align_bytes=64)
         w_scales = keep.tile([P, FEATURES], U8, align_bytes=64)
         xq_codes = keep.tile([P, N_TILES, P], U32, align_bytes=64)
@@ -75,7 +77,9 @@ def tile_avey_pa_kernel(tc, x, g, W1_words, W1_scales, b1, out_0, out_1, out_2):
         floor = keep.tile([P, 1], F32)
         neg_floor = keep.tile([P, 1], F32)
 
+        nc.vector.memset(bias_row[:].bitcast(I32), 0)
         nc.vector.memset(w_scales[:].bitcast(I32), 0)
+        nc.vector.memset(ones[:], 1.0)
         nc.vector.memset(eps_rms[:], EPS_RMS)
         nc.vector.memset(floor[:], EPS_NORM * EPS_NORM)
         nc.vector.memset(neg_floor[:], -EPS_NORM * EPS_NORM)
@@ -93,15 +97,15 @@ def tile_avey_pa_kernel(tc, x, g, W1_words, W1_scales, b1, out_0, out_1, out_2):
                 in_=w_bytes[:, PACK * first : PACK * end].bitcast(I32),
             )
 
-        nc.scalar.dma_start(out=bias[:], in_=b1.partition_broadcast(P))
         load_x(X_PIECES[0])
         nc.sync.dma_start(out=gain[:], in_=g.rearrange("(q t) -> q t", t=PACK))
+        nc.sync.dma_start(out=bias_row[0:1, :], in_=b1.unsqueeze(0))
+        load_x(X_PIECES[1])
         for quadrant in range(4):
             nc.sync.dma_start(
                 out=w_scales[32 * quadrant : 32 * quadrant + 4, :].bitcast(I32),
                 in_=w_scale_rows[4 * quadrant : 4 * quadrant + 4, :].bitcast(I32),
             )
-        load_x(X_PIECES[1])
         load_w(RIGHT)
         load_x(X_PIECES[2])
         load_w(HEAD_PART)
@@ -284,15 +288,28 @@ def tile_avey_pa_kernel(tc, x, g, W1_words, W1_scales, b1, out_0, out_1, out_2):
                 bias=floor[:],
             )
 
+        spread = {}
+
+        def spread_bias(start):
+            spread[start] = acc_banks.tile([P, BANK], F32, name="acc")
+            nc.tensor.matmul(
+                out=spread[start][:], lhsT=ones[:], rhs=bias_row[:, start : start + BANK], start=True, stop=True
+            )
+
+        spread_bias(R0)
         mean_square(0)
         reciprocal_rms(0, 1)
         scale_rows_vector(0)
         flip(0)
+        spread_bias(0)
         mean_square(1)
         reciprocal_rms(1, 2)
         scale_rows_vector(1)
         flip(1)
+        spread_bias(BANK)
+        spread_bias(L0)
         apply_gain(0)
+        nc.vector.tensor_copy(out=bias[:, R0 : R0 + BANK], in_=spread[R0][:])
         mean_square(2)
         mean_square(3)
         reciprocal_rms(2, 4)
@@ -300,6 +317,8 @@ def tile_avey_pa_kernel(tc, x, g, W1_words, W1_scales, b1, out_0, out_1, out_2):
         quantise(0)
         apply_gain(1)
         scale_rows_scalar(3)
+        for start in (0, BANK, L0):
+            nc.scalar.copy(out=bias[:, start : start + BANK], in_=spread[start][:])
 
         LAST = N_TILES - 1
         for i in range(N_TILES):

@@ -313,19 +313,37 @@ def tile_avey_pa_kernel(tc, x, g, W1_words, W1_scales, b1, out_0, out_1, out_2):
         mean_square(2)
         mean_square(3)
         reciprocal_rms(2, 4)
-        scale_rows_vector(2)
         quantise(0)
+        scale_rows_vector(2)
         apply_gain(1)
         scale_rows_scalar(3)
         for start in (0, BANK, L0):
             nc.scalar.copy(out=bias[:, start : start + BANK], in_=spread[start][:])
 
         LAST = N_TILES - 1
+        BY_VECTOR = {LAST - 1: (BANK, L0), LAST: (BANK, L0)}
+        WIDE_BANKS = (0, BANK, L0)
+
+        def finish_store(i, start):
+            if start == BANK or (start == 0 and BANK in BY_VECTOR.get(i, ())):
+                store_head(i)
+            if start == L0:
+                store_left(i)
+
+        waiting = []
+
+        def square_one_waiting():
+            if waiting:
+                j, start = waiting[0]
+                waiting.remove((j, start))
+                square(pre[(j, WIDE)][:, start : start + BANK])
+                finish_store(j, start)
+
         for i in range(N_TILES):
             pre[(i, RIGHT)] = results.tile([P, HALF], F32, name="pre_right")
             pre[(i, WIDE)] = results.tile([P, HEAD + HALF], F32, name="pre_wide")
             wide = pre[(i, WIDE)]
-            before = pre.get((i - 1, WIDE))
+            own = BY_VECTOR.get(i, ())
             product(i, R0)
             add_bias(i, RIGHT, R0)
             product(i, 0)
@@ -345,30 +363,21 @@ def tile_avey_pa_kernel(tc, x, g, W1_words, W1_scales, b1, out_0, out_1, out_2):
                 scale_rows_one_port(i + 3)
             if i < LAST:
                 relu_pool(pre[(i, RIGHT)][:])
+            rest = [start for start in WIDE_BANKS if start not in own]
+            if i == LAST:
+                relu_pool(wide[:, rest[0] : rest[-1] + BANK])
             if i > 0:
                 normalise_right_pool(i - 1)
             if i < LAST:
-                relu_pool(wide[:])
-            else:
-                relu_pool(wide[:, 0:BANK])
-            if i > 0:
-                square(before[:, 0:BANK])
+                relu_pool(wide[:, rest[0] : rest[-1] + BANK])
+            square_one_waiting()
             if i < LAST:
                 square(pre[(i, RIGHT)][:])
-            else:
-                sum_fourth(i)
-            if i > 0:
-                square(before[:, BANK : 2 * BANK])
-                store_head(i - 1)
-            if i < LAST:
-                sum_fourth(i)
-            else:
-                floor_sum(i)
-            if i > 0:
-                square(before[:, HEAD : HEAD + HALF])
-                store_left(i - 1)
-            if i < LAST:
-                floor_sum(i)
+                square_one_waiting()
+            sum_fourth(i)
+            square_one_waiting()
+            floor_sum(i)
+            square_one_waiting()
             if i == 0:
                 mean_square(4)
                 mean_square(5)
@@ -378,10 +387,12 @@ def tile_avey_pa_kernel(tc, x, g, W1_words, W1_scales, b1, out_0, out_1, out_2):
                 mean_square(7)
                 reciprocal_rms(6, 8)
             inverse_norm(i)
-            if i == LAST:
-                squared_relu_vector(wide[:, BANK : 2 * BANK])
-                squared_relu_vector(wide[:, HEAD : HEAD + HALF])
-                store_left(i)
-                square(wide[:, 0:BANK])
-                store_head(i)
-                normalise_right_vector(i)
+            for start in own:
+                squared_relu_vector(wide[:, start : start + BANK])
+                if start == L0:
+                    store_left(i)
+            for start in rest:
+                waiting.extend([(i, start)])
+        for start in WIDE_BANKS:
+            square_one_waiting()
+        normalise_right_vector(LAST)

@@ -356,6 +356,8 @@ def tile_avey_pa_kernel(tc, x, g, W1_words, W1_scales, b1, out_0, out_1, out_2):
             add_bias_wide(i, L0)
             if i + 1 < N_TILES:
                 quantise(i + 1)
+            if i > 1:
+                normalise_right_vector(i - 2)
             if i + 2 < N_TILES:
                 flip(i + 2)
                 apply_gain(i + 2)
@@ -364,12 +366,7 @@ def tile_avey_pa_kernel(tc, x, g, W1_words, W1_scales, b1, out_0, out_1, out_2):
             if i < LAST:
                 relu_pool(pre[(i, RIGHT)][:])
             rest = [start for start in WIDE_BANKS if start not in own]
-            if i == LAST:
-                relu_pool(wide[:, rest[0] : rest[-1] + BANK])
-            if i > 0:
-                normalise_right_pool(i - 1)
-            if i < LAST:
-                relu_pool(wide[:, rest[0] : rest[-1] + BANK])
+            relu_pool(wide[:, rest[0] : rest[-1] + BANK])
             square_one_waiting()
             if i < LAST:
                 square(pre[(i, RIGHT)][:])
@@ -395,4 +392,5 @@ def tile_avey_pa_kernel(tc, x, g, W1_words, W1_scales, b1, out_0, out_1, out_2):
                 waiting.extend([(i, start)])
         for start in WIDE_BANKS:
             square_one_waiting()
+        normalise_right_vector(LAST - 1)
         normalise_right_vector(LAST)

@@ -358,11 +358,11 @@ def tile_avey_pa_kernel(tc, x, g, W1_words, W1_scales, b1, out_0, out_1, out_2):
                 quantise(i + 1)
             if i > 1:
                 normalise_right_vector(i - 2)
+            if 4 <= i + 3 < N_TILES:
+                scale_rows_vector(i + 3)
             if i + 2 < N_TILES:
                 flip(i + 2)
                 apply_gain(i + 2)
-            if 4 <= i + 3 < N_TILES:
-                scale_rows_one_port(i + 3)
             if i < LAST:
                 relu_pool(pre[(i, RIGHT)][:])
             rest = [start for start in WIDE_BANKS if start not in own]

@@ -21,28 +21,30 @@ HALF = 512
 FEATURES = HEAD + 2 * HALF
 BANK = 512
 N_TILES = TOKENS // P
+LAST = N_TILES - 1
 EPS_RMS = 1e-6
 EPS_NORM = 1e-12
 FLT_BIG = 3.0e38
 
 FLOPS = 2 * TOKENS * K * FEATURES
 
+LEFT = HEAD
+RIGHT = HEAD + HALF
+WIDE = HEAD + HALF
+WIDE_BANKS = (0, BANK, LEFT)
+
 X_PIECES = ((0, 1), (1, 2), (2, 4), (4, 8))
-RIGHT = (HEAD + HALF, FEATURES)
-HEAD_PART = (0, HEAD)
-LEFT = (HEAD, HEAD + HALF)
-PARTS = (RIGHT, HEAD_PART, LEFT)
+SCALED_AT_HEAD = 4
+BY_VECTOR = {LAST - 1: (BANK, LEFT), LAST: (BANK, LEFT)}
 
 
 def tile_avey_pa_kernel(tc, x, g, W1_words, W1_scales, b1, out_0, out_1, out_2):
     nc = tc.nc
 
     x_rows = x.flatten_outer_dims().rearrange("(p i) k -> p i k", i=N_TILES)
-    out_rows = {
-        RIGHT: out_2.flatten_outer_dims().rearrange("(p i) n -> p i n", i=N_TILES),
-        HEAD_PART: out_0.flatten_outer_dims().rearrange("(p i) n -> p i n", i=N_TILES),
-        LEFT: out_1.flatten_outer_dims().rearrange("(p i) n -> p i n", i=N_TILES),
-    }
+    right_rows = out_2.flatten_outer_dims().rearrange("(p i) n -> p i n", i=N_TILES)
+    head_rows = out_0.flatten_outer_dims().rearrange("(p i) n -> p i n", i=N_TILES)
+    left_rows = out_1.flatten_outer_dims().rearrange("(p i) n -> p i n", i=N_TILES)
     w_bytes = W1_words.rearrange("o p n t -> p (o n t)")
     w_scale_rows = W1_scales.rearrange("o q n -> (o q) n")
 
@@ -71,9 +73,8 @@ def tile_avey_pa_kernel(tc, x, g, W1_words, W1_scales, b1, out_0, out_1, out_2):
         sum_sq = keep.tile([P, N_TILES], F32)
         rstd = keep.tile([P, N_TILES], F32)
         right_sq = keep.tile([P, N_TILES], F32)
-        right_rsqrt = keep.tile([P, N_TILES], F32)
+        right_floored = keep.tile([P, N_TILES], F32)
         right_inv = keep.tile([P, N_TILES], F32)
-        unused_sum = keep.tile([P, N_TILES], F32)
         floor = keep.tile([P, 1], F32)
         neg_floor = keep.tile([P, 1], F32)
 
@@ -86,12 +87,12 @@ def tile_avey_pa_kernel(tc, x, g, W1_words, W1_scales, b1, out_0, out_1, out_2):
         nc.scalar.activation(out=table_warm[:], in_=eps_rms[:], func=ACT.Abs_reciprocal_sqrt)
         make_identity(nc, identity[:])
 
+
         def load_x(piece):
             first, end = piece
             nc.sync.dma_start(out=x_sb[:, first:end, :], in_=x_rows[:, first:end, :])
 
-        def load_w(part):
-            first, end = part
+        def load_w(first, end):
             nc.sync.dma_start(
                 out=w_codes[:, first:end].bitcast(I32),
                 in_=w_bytes[:, PACK * first : PACK * end].bitcast(I32),
@@ -106,13 +107,14 @@ def tile_avey_pa_kernel(tc, x, g, W1_words, W1_scales, b1, out_0, out_1, out_2):
                 out=w_scales[32 * quadrant : 32 * quadrant + 4, :].bitcast(I32),
                 in_=w_scale_rows[4 * quadrant : 4 * quadrant + 4, :].bitcast(I32),
             )
-        load_w(RIGHT)
+        load_w(RIGHT, FEATURES)
         load_x(X_PIECES[2])
-        load_w(HEAD_PART)
-        load_w(LEFT)
+        load_w(0, HEAD)
+        load_w(LEFT, RIGHT)
         load_x(X_PIECES[3])
 
-        def mean_square(i):
+
+        def sum_squares(i):
             squares = work.tile([P, K], BF16)
             nc.scalar.activation(
                 out=squares[:], in_=x_sb[:, i, :], func=ACT.Square, accum_out=sum_sq[:, i : i + 1]
@@ -127,25 +129,14 @@ def tile_avey_pa_kernel(tc, x, g, W1_words, W1_scales, b1, out_0, out_1, out_2):
                 bias=eps_rms[:],
             )
 
-        def scale_rows_vector(i):
+        def scale_rows(i):
             nc.vector.tensor_scalar_mul(
                 out=scaled[:, i, :, :],
                 in0=x_sb[:, i, :].rearrange("p (q t) -> p t q", t=PACK),
                 scalar1=rstd[:, i : i + 1],
             )
 
-        def scale_rows_one_port(i):
-            nc.vector.tensor_scalar(
-                out=scaled[:, i, :, :],
-                in0=x_sb[:, i, :].rearrange("p (q t) -> p t q", t=PACK),
-                scalar1=rstd[:, i : i + 1],
-                scalar2=None,
-                op0=ALU.mult,
-                op1=ALU.add,
-                accum_out=unused_sum[:, i : i + 1],
-            )
-
-        def scale_rows_scalar(i):
+        def scale_rows_on_scalar(i):
             nc.scalar.activation(
                 out=scaled[:, i, :, :],
                 in_=x_sb[:, i, :].rearrange("p (q t) -> p t q", t=PACK),
@@ -175,14 +166,15 @@ def tile_avey_pa_kernel(tc, x, g, W1_words, W1_scales, b1, out_0, out_1, out_2):
                 in_=grouped[:, i, :, :].rearrange("q r t -> q (r t)"),
             )
 
-        pre = {}
-        accs = {}
+        right = {}
+        wide = {}
+        acc = {}
 
         def product(i, start):
             cols = slice(start, start + BANK)
-            accs[(i, start)] = acc_banks.tile([P, BANK], F32, name="acc")
+            acc[(i, start)] = acc_banks.tile([P, BANK], F32, name="acc")
             nc.tensor.matmul_mx(
-                out=accs[(i, start)][:],
+                out=acc[(i, start)][:],
                 lhsT=xq_codes[:, i, :].bitcast(FP8X4),
                 lhsT_scale=xq_scales[:, i, :],
                 rhs=w_codes[:, cols].bitcast(FP8X4),
@@ -191,102 +183,54 @@ def tile_avey_pa_kernel(tc, x, g, W1_words, W1_scales, b1, out_0, out_1, out_2):
                 stop=True,
             )
 
-        def add_bias(i, part, start):
-            first = part[0]
+        def product_plus_bias(i, start):
+            product(i, start)
+            target = right[i][:, 0:BANK] if start == RIGHT else wide[i][:, start : start + BANK]
             nc.vector.tensor_tensor(
-                out=pre[(i, part)][:, start - first : start - first + BANK],
-                in0=accs[(i, start)][:],
-                in1=bias[:, start : start + BANK],
-                op=ALU.add,
+                out=target, in0=acc[(i, start)][:], in1=bias[:, start : start + BANK], op=ALU.add
             )
 
-        def relu_pool(view):
+        def relu(view):
             nc.gpsimd.tensor_scalar(
                 out=view, in0=view, scalar1=FLT_BIG, scalar2=0.0, op0=ALU.min, op1=ALU.max
-            )
-
-        def squared_relu_vector(view):
-            nc.vector.scalar_tensor_tensor(
-                out=view, in0=view, scalar=0.0, in1=view, op0=ALU.max, op1=ALU.mult
             )
 
         def square(view):
             nc.scalar.activation(out=view, in_=view, func=ACT.Square)
 
-        def right_norm(i):
-            fourth = work.tile([P, HALF], F32)
-            nc.scalar.activation(
-                out=fourth[:], in_=pre[(i, RIGHT)][:], func=ACT.Square, accum_out=right_sq[:, i : i + 1]
-            )
-            nc.scalar.activation(
-                out=right_rsqrt[:, i : i + 1],
-                in_=right_sq[:, i : i + 1],
-                func=ACT.Relu,
-                bias=neg_floor[:],
-            )
-            nc.scalar.activation(
-                out=right_inv[:, i : i + 1],
-                in_=right_rsqrt[:, i : i + 1],
-                func=ACT.Abs_reciprocal_sqrt,
-                bias=floor[:],
-            )
-
-        def store(i, part):
-            nc.sync.dma_start(out=out_rows[part][:, i, :], in_=pre[(i, part)][:])
-
-        def normalise_right_pool(i):
-            nc.gpsimd.tensor_scalar(
-                out=pre[(i, RIGHT)][:],
-                in0=pre[(i, RIGHT)][:],
-                scalar1=right_inv[:, i : i + 1],
-                scalar2=1.0,
-                op0=ALU.mult,
-                op1=ALU.mult,
-            )
-            store(i, RIGHT)
-
-        def normalise_right_vector(i):
-            nc.vector.tensor_scalar_mul(
-                out=pre[(i, RIGHT)][:], in0=pre[(i, RIGHT)][:], scalar1=right_inv[:, i : i + 1]
-            )
-            store(i, RIGHT)
-
-        R0 = RIGHT[0]
-        L0 = LEFT[0]
-        WIDE = (0, HEAD + HALF)
-
-        def add_bias_wide(i, start):
-            nc.vector.tensor_tensor(
-                out=pre[(i, WIDE)][:, start : start + BANK],
-                in0=accs[(i, start)][:],
-                in1=bias[:, start : start + BANK],
-                op=ALU.add,
+        def squared_relu(view):
+            nc.vector.scalar_tensor_tensor(
+                out=view, in0=view, scalar=0.0, in1=view, op0=ALU.max, op1=ALU.mult
             )
 
         def store_head(i):
-            nc.sync.dma_start(out=out_rows[HEAD_PART][:, i, :], in_=pre[(i, WIDE)][:, 0:HEAD])
+            nc.sync.dma_start(out=head_rows[:, i, :], in_=wide[i][:, 0:HEAD])
 
         def store_left(i):
-            nc.sync.dma_start(out=out_rows[LEFT][:, i, :], in_=pre[(i, WIDE)][:, HEAD : HEAD + HALF])
+            nc.sync.dma_start(out=left_rows[:, i, :], in_=wide[i][:, HEAD : HEAD + HALF])
 
         def sum_fourth(i):
             fourth = work.tile([P, HALF], F32)
             nc.scalar.activation(
-                out=fourth[:], in_=pre[(i, RIGHT)][:], func=ACT.Square, accum_out=right_sq[:, i : i + 1]
+                out=fourth[:], in_=right[i][:], func=ACT.Square, accum_out=right_sq[:, i : i + 1]
             )
 
         def floor_sum(i):
             nc.scalar.activation(
-                out=right_rsqrt[:, i : i + 1], in_=right_sq[:, i : i + 1], func=ACT.Relu, bias=neg_floor[:]
+                out=right_floored[:, i : i + 1], in_=right_sq[:, i : i + 1], func=ACT.Relu, bias=neg_floor[:]
             )
 
-        def inverse_norm(i):
+        def reciprocal_norm(i):
             nc.scalar.activation(
                 out=right_inv[:, i : i + 1],
-                in_=right_rsqrt[:, i : i + 1],
+                in_=right_floored[:, i : i + 1],
                 func=ACT.Abs_reciprocal_sqrt,
                 bias=floor[:],
             )
+
+        def normalise_right(i):
+            nc.vector.tensor_scalar_mul(out=right[i][:], in0=right[i][:], scalar1=right_inv[:, i : i + 1])
+            nc.sync.dma_start(out=right_rows[:, i, :], in_=right[i][:])
 
         spread = {}
 
@@ -296,39 +240,30 @@ def tile_avey_pa_kernel(tc, x, g, W1_words, W1_scales, b1, out_0, out_1, out_2):
                 out=spread[start][:], lhsT=ones[:], rhs=bias_row[:, start : start + BANK], start=True, stop=True
             )
 
-        spread_bias(R0)
-        mean_square(0)
+        spread_bias(RIGHT)
+        sum_squares(0)
         reciprocal_rms(0, 1)
-        scale_rows_vector(0)
+        scale_rows(0)
         flip(0)
         spread_bias(0)
-        mean_square(1)
+        sum_squares(1)
         reciprocal_rms(1, 2)
-        scale_rows_vector(1)
+        scale_rows(1)
         flip(1)
         spread_bias(BANK)
-        spread_bias(L0)
+        spread_bias(LEFT)
         apply_gain(0)
-        nc.vector.tensor_copy(out=bias[:, R0 : R0 + BANK], in_=spread[R0][:])
-        mean_square(2)
-        mean_square(3)
+        nc.vector.tensor_copy(out=bias[:, RIGHT : RIGHT + BANK], in_=spread[RIGHT][:])
+        sum_squares(2)
+        sum_squares(3)
         reciprocal_rms(2, 4)
         quantise(0)
-        scale_rows_vector(2)
+        scale_rows(2)
         apply_gain(1)
-        scale_rows_scalar(3)
-        for start in (0, BANK, L0):
+        scale_rows_on_scalar(3)
+        for start in WIDE_BANKS:
             nc.scalar.copy(out=bias[:, start : start + BANK], in_=spread[start][:])
 
-        LAST = N_TILES - 1
-        BY_VECTOR = {LAST - 1: (BANK, L0), LAST: (BANK, L0)}
-        WIDE_BANKS = (0, BANK, L0)
-
-        def finish_store(i, start):
-            if start == BANK or (start == 0 and BANK in BY_VECTOR.get(i, ())):
-                store_head(i)
-            if start == L0:
-                store_left(i)
 
         waiting = []
 
@@ -336,61 +271,60 @@ def tile_avey_pa_kernel(tc, x, g, W1_words, W1_scales, b1, out_0, out_1, out_2):
             if waiting:
                 j, start = waiting[0]
                 waiting.remove((j, start))
-                square(pre[(j, WIDE)][:, start : start + BANK])
-                finish_store(j, start)
+                square(wide[j][:, start : start + BANK])
+                if start == BANK or (start == 0 and BANK in BY_VECTOR.get(j, ())):
+                    store_head(j)
+                if start == LEFT:
+                    store_left(j)
 
         for i in range(N_TILES):
-            pre[(i, RIGHT)] = results.tile([P, HALF], F32, name="pre_right")
-            pre[(i, WIDE)] = results.tile([P, HEAD + HALF], F32, name="pre_wide")
-            wide = pre[(i, WIDE)]
+            right[i] = results.tile([P, HALF], F32, name="pre_right")
+            wide[i] = results.tile([P, WIDE], F32, name="pre_wide")
             own = BY_VECTOR.get(i, ())
-            product(i, R0)
-            add_bias(i, RIGHT, R0)
-            product(i, 0)
-            add_bias_wide(i, 0)
+            rest = [start for start in WIDE_BANKS if start not in own]
+
+            product_plus_bias(i, RIGHT)
+            product_plus_bias(i, 0)
             if i == LAST:
-                squared_relu_vector(pre[(i, RIGHT)][:])
-            product(i, BANK)
-            add_bias_wide(i, BANK)
-            product(i, L0)
-            add_bias_wide(i, L0)
+                squared_relu(right[i][:])
+            product_plus_bias(i, BANK)
+            product_plus_bias(i, LEFT)
             if i + 1 < N_TILES:
                 quantise(i + 1)
             if i > 1:
-                normalise_right_vector(i - 2)
-            if 4 <= i + 3 < N_TILES:
-                scale_rows_vector(i + 3)
+                normalise_right(i - 2)
+            if SCALED_AT_HEAD <= i + 3 < N_TILES:
+                scale_rows(i + 3)
             if i + 2 < N_TILES:
                 flip(i + 2)
                 apply_gain(i + 2)
+
             if i < LAST:
-                relu_pool(pre[(i, RIGHT)][:])
-            rest = [start for start in WIDE_BANKS if start not in own]
-            relu_pool(wide[:, rest[0] : rest[-1] + BANK])
+                relu(right[i][:])
+            relu(wide[i][:, rest[0] : rest[-1] + BANK])
+
             square_one_waiting()
             if i < LAST:
-                square(pre[(i, RIGHT)][:])
+                square(right[i][:])
                 square_one_waiting()
             sum_fourth(i)
             square_one_waiting()
             floor_sum(i)
             square_one_waiting()
-            if i == 0:
-                mean_square(4)
-                mean_square(5)
-                reciprocal_rms(4, 6)
-            if i == 1:
-                mean_square(6)
-                mean_square(7)
-                reciprocal_rms(6, 8)
-            inverse_norm(i)
+            if i < 2:
+                first = SCALED_AT_HEAD + 2 * i
+                sum_squares(first)
+                sum_squares(first + 1)
+                reciprocal_rms(first, first + 2)
+            reciprocal_norm(i)
+
             for start in own:
-                squared_relu_vector(wide[:, start : start + BANK])
-                if start == L0:
+                squared_relu(wide[i][:, start : start + BANK])
+                if start == LEFT:
                     store_left(i)
-            for start in rest:
-                waiting.extend([(i, start)])
+            waiting.extend([(i, start) for start in rest])
+
         for start in WIDE_BANKS:
             square_one_waiting()
-        normalise_right_vector(LAST - 1)
-        normalise_right_vector(LAST)
+        normalise_right(LAST - 1)
+        normalise_right(LAST)

@@ -53,18 +53,21 @@ def tile_avey_pa_kernel(tc, x, g, W1_words, W1_scales, b1, out_0, out_1, out_2):
         keep = stack.enter_context(tc.tile_pool(name="keep", bufs=1))
         work = stack.enter_context(tc.tile_pool(name="work", bufs=3))
         results = stack.enter_context(tc.tile_pool(name="results", bufs=N_TILES))
-        flip_banks = stack.enter_context(tc.psum_pool(name="flip_banks", bufs=2))
+        gain_bank = stack.enter_context(tc.psum_pool(name="gain_bank", bufs=1))
+        flip_banks = stack.enter_context(tc.psum_pool(name="flip_banks", bufs=1))
         acc_banks = stack.enter_context(tc.psum_pool(name="acc_banks", bufs=6))
 
         x_sb = keep.tile([P, N_TILES, K], BF16)
-        scaled = keep.tile([P, N_TILES, PACK, P], F32)
+        xn = keep.tile([P, N_TILES, K], BF16)
+        gained = keep.tile([P, P, PACK], F32)
         grouped = keep.tile([P, N_TILES, P, PACK], BF16, align_bytes=64)
         gain = keep.tile([P, PACK], BF16)
         bias = keep.tile([P, FEATURES], BF16)
         bias_row = keep.tile([P, FEATURES], BF16)
+        gain_row = keep.tile([P, K], BF16)
         ones = keep.tile([P, P], BF16)
         w_codes = keep.tile([P, FEATURES], U32, align_bytes=64)
-        w_scales = keep.tile([P, FEATURES], U8, align_bytes=64)
+        w_scales = keep.tile([P, BANK], U8, align_bytes=64)
         xq_codes = keep.tile([P, N_TILES, P], U32, align_bytes=64)
         xq_scales = keep.tile([P, N_TILES, P], U8, align_bytes=64)
         identity = keep.tile([P, P], F32)
@@ -78,14 +81,16 @@ def tile_avey_pa_kernel(tc, x, g, W1_words, W1_scales, b1, out_0, out_1, out_2):
         floor = keep.tile([P, 1], F32)
         neg_floor = keep.tile([P, 1], F32)
 
-        nc.vector.memset(bias_row[:].bitcast(I32), 0)
-        nc.vector.memset(w_scales[:].bitcast(I32), 0)
-        nc.vector.memset(ones[:], 1.0)
         nc.vector.memset(eps_rms[:], EPS_RMS)
+        nc.vector.memset(gain_row[:].bitcast(I32), 0)
+        nc.vector.memset(bias_row[:, LEFT:].bitcast(I32), 0)
+        nc.vector.memset(ones[:], 1.0)
+        nc.vector.memset(w_scales[:].bitcast(I32), 0)
         nc.vector.memset(floor[:], EPS_NORM * EPS_NORM)
         nc.vector.memset(neg_floor[:], -EPS_NORM * EPS_NORM)
         nc.scalar.activation(out=table_warm[:], in_=eps_rms[:], func=ACT.Abs_reciprocal_sqrt)
         make_identity(nc, identity[:])
+        nc.gpsimd.memset(bias_row[:, 0:LEFT].bitcast(F32), 0.0)
 
 
         def load_x(piece):
@@ -100,14 +105,18 @@ def tile_avey_pa_kernel(tc, x, g, W1_words, W1_scales, b1, out_0, out_1, out_2):
 
         load_x(X_PIECES[0])
         nc.sync.dma_start(out=gain[:], in_=g.rearrange("(q t) -> q t", t=PACK))
-        nc.sync.dma_start(out=bias_row[0:1, :], in_=b1.unsqueeze(0))
+        nc.sync.dma_start(out=gain_row[0:1, :], in_=g.unsqueeze(0))
         load_x(X_PIECES[1])
+        nc.sync.dma_start(out=bias_row[0:1, LEFT:], in_=b1.unsqueeze(0)[:, LEFT:])
         for quadrant in range(4):
             nc.sync.dma_start(
-                out=w_scales[32 * quadrant : 32 * quadrant + 4, :].bitcast(I32),
-                in_=w_scale_rows[4 * quadrant : 4 * quadrant + 4, :].bitcast(I32),
+                out=w_scales[32 * quadrant : 32 * quadrant + 16, :].bitcast(I32),
+                in_=w_scale_rows[4 * quadrant : 4 * quadrant + 4, :]
+                .rearrange("r (j n) -> j r n", n=BANK)
+                .bitcast(I32),
             )
         load_w(RIGHT, FEATURES)
+        nc.sync.dma_start(out=bias_row[0:1, 0:LEFT], in_=b1.unsqueeze(0)[:, 0:LEFT])
         load_x(X_PIECES[2])
         load_w(0, HEAD)
         load_w(LEFT, RIGHT)
@@ -129,34 +138,28 @@ def tile_avey_pa_kernel(tc, x, g, W1_words, W1_scales, b1, out_0, out_1, out_2):
                 bias=eps_rms[:],
             )
 
-        def scale_rows(i):
-            nc.vector.tensor_scalar_mul(
-                out=scaled[:, i, :, :],
-                in0=x_sb[:, i, :].rearrange("p (q t) -> p t q", t=PACK),
-                scalar1=rstd[:, i : i + 1],
-            )
-
-        def scale_rows_on_scalar(i):
-            nc.scalar.activation(
-                out=scaled[:, i, :, :],
-                in_=x_sb[:, i, :].rearrange("p (q t) -> p t q", t=PACK),
-                func=ACT.Copy,
-                scale=rstd[:, i : i + 1],
+        def normalise_rows(i):
+            nc.vector.scalar_tensor_tensor(
+                out=xn[:, i, :],
+                in0=x_sb[:, i, :],
+                scalar=rstd[:, i : i + 1],
+                in1=gain_spread[:],
+                op0=ALU.mult,
+                op1=ALU.mult,
             )
 
         flipped = {}
 
-        def flip(i):
-            flipped[i] = flip_banks.tile([P, PACK, P], F32, name="flipped")
-            for t in range(PACK):
-                nc.tensor.transpose(flipped[i][:, t, :], scaled[:, i, t, :], identity[:])
+        def flip(rows, i):
+            flipped[i] = flip_banks.tile([P, 2, P], F32, name="flipped")
+            words = rows[:, i, :].bitcast(F32)
+            for u in range(2):
+                nc.tensor.transpose(flipped[i][:, u, :], words[:, u::2], identity[:])
 
-        def apply_gain(i):
-            nc.vector.tensor_tensor(
-                out=grouped[:, i, :, :],
-                in0=flipped[i][:].rearrange("q t r -> q r t"),
-                in1=gain[:].unsqueeze(1).to_broadcast([P, P, PACK]),
-                op=ALU.mult,
+        def group(copy, i):
+            copy(
+                out=grouped[:, i, :, :].bitcast(F32),
+                in_=flipped[i][:].rearrange("q u r -> q r u"),
             )
 
         def quantise(i):
@@ -178,17 +181,20 @@ def tile_avey_pa_kernel(tc, x, g, W1_words, W1_scales, b1, out_0, out_1, out_2):
                 lhsT=xq_codes[:, i, :].bitcast(FP8X4),
                 lhsT_scale=xq_scales[:, i, :],
                 rhs=w_codes[:, cols].bitcast(FP8X4),
-                rhs_scale=w_scales[:, cols],
+                rhs_scale=w_scales[PACK * (start // BANK) :, :],
                 start=True,
                 stop=True,
             )
 
-        def product_plus_bias(i, start):
-            product(i, start)
+        def add_bias(i, start):
             target = right[i][:, 0:BANK] if start == RIGHT else wide[i][:, start : start + BANK]
             nc.vector.tensor_tensor(
                 out=target, in0=acc[(i, start)][:], in1=bias[:, start : start + BANK], op=ALU.add
             )
+
+        def product_plus_bias(i, start):
+            product(i, start)
+            add_bias(i, start)
 
         def relu(view):
             nc.gpsimd.tensor_scalar(
@@ -235,34 +241,70 @@ def tile_avey_pa_kernel(tc, x, g, W1_words, W1_scales, b1, out_0, out_1, out_2):
         spread = {}
 
         def spread_bias(start):
-            spread[start] = acc_banks.tile([P, BANK], F32, name="acc")
-            nc.tensor.matmul(
-                out=spread[start][:], lhsT=ones[:], rhs=bias_row[:, start : start + BANK], start=True, stop=True
-            )
+            spread[start] = acc_banks.tile([P, 2 * BANK], BF16, name="acc")
+            for half in (0, BANK):
+                nc.tensor.matmul(
+                    out=spread[start][:, half : half + BANK],
+                    lhsT=ones[:],
+                    rhs=bias_row[:, start + half : start + half + BANK],
+                    start=True,
+                    stop=True,
+                )
 
-        spread_bias(RIGHT)
+        flip(x_sb, 0)
+        nc.vector.tensor_tensor(
+            out=gained[:].rearrange("q r (u e) -> q r u e", u=2),
+            in0=flipped[0][:].rearrange("q u r -> q (u r)").bitcast(BF16).rearrange("q (u r e) -> q r u e", u=2, e=2),
+            in1=gain[:].rearrange("q (u e) -> q u e", u=2).unsqueeze(1).to_broadcast([P, P, 2, 2]),
+            op=ALU.mult,
+        )
         sum_squares(0)
         reciprocal_rms(0, 1)
-        scale_rows(0)
-        flip(0)
-        spread_bias(0)
+        gain_spread = gain_bank.tile([P, K], F32, name="gain_spread")
+        nc.tensor.matmul(out=gain_spread[:], lhsT=ones[:], rhs=gain_row[:], start=True, stop=True)
+        rstd_spread = acc_banks.tile([P, P], F32, name="acc")
+        nc.tensor.matmul(
+            out=rstd_spread[:], lhsT=rstd[:, 0:1].to_broadcast([P, P]), rhs=identity[:], start=True, stop=True
+        )
+        nc.vector.tensor_tensor(
+            out=grouped[:, 0, :, :],
+            in0=gained[:],
+            in1=rstd_spread[:].unsqueeze(2).to_broadcast([P, P, PACK]),
+            op=ALU.mult,
+        )
         sum_squares(1)
         reciprocal_rms(1, 2)
-        scale_rows(1)
-        flip(1)
-        spread_bias(BANK)
         spread_bias(LEFT)
-        apply_gain(0)
-        nc.vector.tensor_copy(out=bias[:, RIGHT : RIGHT + BANK], in_=spread[RIGHT][:])
-        sum_squares(2)
-        sum_squares(3)
-        reciprocal_rms(2, 4)
+        nc.scalar.copy(out=bias[:, RIGHT:FEATURES], in_=spread[LEFT][:, BANK : 2 * BANK])
         quantise(0)
-        scale_rows(2)
-        apply_gain(1)
-        scale_rows_on_scalar(3)
-        for start in WIDE_BANKS:
-            nc.scalar.copy(out=bias[:, start : start + BANK], in_=spread[start][:])
+        normalise_rows(1)
+        sum_squares(2)
+        nc.vector.tensor_copy(out=bias[:, LEFT:RIGHT], in_=spread[LEFT][:, 0:BANK])
+
+        right[0] = results.tile([P, HALF], F32, name="pre_right")
+        wide[0] = results.tile([P, WIDE], F32, name="pre_wide")
+        product(0, RIGHT)
+        spread_bias(0)
+        flip(xn, 1)
+        product(0, 0)
+        product(0, BANK)
+        add_bias(0, RIGHT)
+        nc.scalar.copy(out=bias[:, 0:BANK], in_=spread[0][:, 0:BANK])
+        reciprocal_rms(2, 3)
+        nc.scalar.copy(out=bias[:, BANK:HEAD], in_=spread[0][:, BANK:HEAD])
+        sum_squares(3)
+        reciprocal_rms(3, 4)
+        relu(right[0][:])
+        group(nc.vector.tensor_copy, 1)
+        add_bias(0, 0)
+        product(0, LEFT)
+        normalise_rows(2)
+        flip(xn, 2)
+        add_bias(0, BANK)
+        quantise(1)
+        add_bias(0, LEFT)
+        relu(wide[0][:])
+        normalise_rows(3)
 
 
         waiting = []
@@ -277,54 +319,72 @@ def tile_avey_pa_kernel(tc, x, g, W1_words, W1_scales, b1, out_0, out_1, out_2):
                 if start == LEFT:
                     store_left(j)
 
+        def finish_on_vector(i):
+            for start in BY_VECTOR[i]:
+                squared_relu(wide[i][:, start : start + BANK])
+            store_left(i)
+
         for i in range(N_TILES):
-            right[i] = results.tile([P, HALF], F32, name="pre_right")
-            wide[i] = results.tile([P, WIDE], F32, name="pre_wide")
             own = BY_VECTOR.get(i, ())
             rest = [start for start in WIDE_BANKS if start not in own]
+            if i > 0:
+                right[i] = results.tile([P, HALF], F32, name="pre_right")
+                wide[i] = results.tile([P, WIDE], F32, name="pre_wide")
 
-            product_plus_bias(i, RIGHT)
-            product_plus_bias(i, 0)
-            if i == LAST:
-                squared_relu(right[i][:])
-            product_plus_bias(i, BANK)
-            product_plus_bias(i, LEFT)
-            if i + 1 < N_TILES:
-                quantise(i + 1)
-            if i > 1:
-                normalise_right(i - 2)
-            if SCALED_AT_HEAD <= i + 3 < N_TILES:
-                scale_rows(i + 3)
-            if i + 2 < N_TILES:
-                flip(i + 2)
-                apply_gain(i + 2)
+                product_plus_bias(i, RIGHT)
+                product_plus_bias(i, 0)
+                if i == LAST:
+                    squared_relu(right[i][:])
+                product_plus_bias(i, BANK)
+                product_plus_bias(i, LEFT)
+                if i + 1 < N_TILES:
+                    quantise(i + 1)
+                if 1 < i < LAST:
+                    normalise_right(i - 2)
+                if i + 3 < N_TILES:
+                    normalise_rows(i + 3)
+                if i + 2 < N_TILES:
+                    flip(xn, i + 2)
 
-            if i < LAST:
-                relu(right[i][:])
-            relu(wide[i][:, rest[0] : rest[-1] + BANK])
+                if i < LAST:
+                    relu(right[i][:])
+                relu(wide[i][:, rest[0] : rest[-1] + BANK])
 
-            square_one_waiting()
-            if i < LAST:
+            if i == LAST - 1:
+                finish_on_vector(i)
+                normalise_right(i - 1)
+
+            if i == 0:
+                sum_squares(4)
+                sum_squares(5)
+                group(nc.scalar.copy, 2)
+                reciprocal_rms(4, 6)
                 square(right[i][:])
+                sum_squares(6)
+                sum_fourth(i)
+                sum_squares(7)
+                floor_sum(i)
+                reciprocal_rms(6, 8)
+                reciprocal_norm(i)
+            else:
                 square_one_waiting()
-            sum_fourth(i)
-            square_one_waiting()
-            floor_sum(i)
-            square_one_waiting()
-            if i < 2:
-                first = SCALED_AT_HEAD + 2 * i
-                sum_squares(first)
-                sum_squares(first + 1)
-                reciprocal_rms(first, first + 2)
-            reciprocal_norm(i)
+                if i < LAST:
+                    square(right[i][:])
+                if i + 2 < N_TILES:
+                    group(nc.scalar.copy, i + 2)
+                if i < LAST:
+                    square_one_waiting()
+                sum_fourth(i)
+                square_one_waiting()
+                floor_sum(i)
+                square_one_waiting()
+                reciprocal_norm(i)
 
-            for start in own:
-                squared_relu(wide[i][:, start : start + BANK])
-                if start == LEFT:
-                    store_left(i)
+            if i == LAST:
+                normalise_right(i - 1)
+                finish_on_vector(i)
             waiting.extend([(i, start) for start in rest])
 
         for start in WIDE_BANKS:
             square_one_waiting()
-        normalise_right(LAST - 1)
         normalise_right(LAST)

@@ -35,6 +35,7 @@ WIDE_BANKS = (0, BANK, LEFT)
 
 X_PIECES = ((0, 1), (1, 2), (2, 4), (4, 8))
 SCALED_AT_HEAD = 4
+WARM_UP = 10
 BY_VECTOR = {LAST - 1: (BANK, LEFT), LAST: (BANK, LEFT)}
 
 
@@ -82,9 +83,9 @@ def tile_avey_pa_kernel(tc, x, g, W1_words, W1_scales, b1, out_0, out_1, out_2):
         neg_floor = keep.tile([P, 1], F32)
 
         nc.vector.memset(eps_rms[:], EPS_RMS)
+        nc.vector.memset(ones[:], 1.0)
         nc.vector.memset(gain_row[:].bitcast(I32), 0)
         nc.vector.memset(bias_row[:, LEFT:].bitcast(I32), 0)
-        nc.vector.memset(ones[:], 1.0)
         nc.vector.memset(w_scales[:].bitcast(I32), 0)
         nc.vector.memset(floor[:], EPS_NORM * EPS_NORM)
         nc.vector.memset(neg_floor[:], -EPS_NORM * EPS_NORM)
@@ -240,17 +241,20 @@ def tile_avey_pa_kernel(tc, x, g, W1_words, W1_scales, b1, out_0, out_1, out_2):
 
         spread = {}
 
-        def spread_bias(start):
-            spread[start] = acc_banks.tile([P, 2 * BANK], BF16, name="acc")
-            for half in (0, BANK):
+        def spread_bias(first, end):
+            spread[first] = acc_banks.tile([P, end - first], BF16, name="acc")
+            for start in range(first, end, BANK):
                 nc.tensor.matmul(
-                    out=spread[start][:, half : half + BANK],
+                    out=spread[first][:, start - first : start - first + BANK],
                     lhsT=ones[:],
-                    rhs=bias_row[:, start + half : start + half + BANK],
+                    rhs=bias_row[:, start : start + BANK],
                     start=True,
                     stop=True,
                 )
 
+        warm_up = acc_banks.tile([P, P], F32, name="acc")
+        for repeat in range(WARM_UP):
+            nc.tensor.matmul(out=warm_up[:], lhsT=ones[:], rhs=ones[:], start=True, stop=True)
         flip(x_sb, 0)
         nc.vector.tensor_tensor(
             out=gained[:].rearrange("q r (u e) -> q r u e", u=2),
@@ -274,18 +278,18 @@ def tile_avey_pa_kernel(tc, x, g, W1_words, W1_scales, b1, out_0, out_1, out_2):
         )
         sum_squares(1)
         reciprocal_rms(1, 2)
-        spread_bias(LEFT)
-        nc.scalar.copy(out=bias[:, RIGHT:FEATURES], in_=spread[LEFT][:, BANK : 2 * BANK])
+        spread_bias(RIGHT, FEATURES)
+        nc.scalar.copy(out=bias[:, RIGHT:FEATURES], in_=spread[RIGHT][:])
         quantise(0)
         normalise_rows(1)
         sum_squares(2)
-        nc.vector.tensor_copy(out=bias[:, LEFT:RIGHT], in_=spread[LEFT][:, 0:BANK])
 
         right[0] = results.tile([P, HALF], F32, name="pre_right")
         wide[0] = results.tile([P, WIDE], F32, name="pre_wide")
         product(0, RIGHT)
-        spread_bias(0)
+        spread_bias(0, LEFT)
         flip(xn, 1)
+        spread_bias(LEFT, RIGHT)
         product(0, 0)
         product(0, BANK)
         add_bias(0, RIGHT)
@@ -296,6 +300,7 @@ def tile_avey_pa_kernel(tc, x, g, W1_words, W1_scales, b1, out_0, out_1, out_2):
         reciprocal_rms(3, 4)
         relu(right[0][:])
         group(nc.vector.tensor_copy, 1)
+        nc.vector.tensor_copy(out=bias[:, LEFT:RIGHT], in_=spread[LEFT][:])
         add_bias(0, 0)
         product(0, LEFT)
         normalise_rows(2)

@@ -33,7 +33,7 @@ RIGHT = HEAD + HALF
 WIDE = HEAD + HALF
 WIDE_BANKS = (0, BANK, LEFT)
 
-X_PIECES = ((0, 1), (1, 2), (2, 4), (4, 8))
+X_PIECES = ((0, 1), (1, 2), (2, 3), (3, 4), (4, 6), (6, 8))
 SCALED_AT_HEAD = 4
 WARM_UP = 10
 BY_VECTOR = {LAST - 1: (BANK, LEFT), LAST: (BANK, LEFT)}
@@ -109,6 +109,7 @@ def tile_avey_pa_kernel(tc, x, g, W1_words, W1_scales, b1, out_0, out_1, out_2):
         nc.sync.dma_start(out=gain_row[0:1, :], in_=g.unsqueeze(0))
         load_x(X_PIECES[1])
         nc.sync.dma_start(out=bias_row[0:1, LEFT:], in_=b1.unsqueeze(0)[:, LEFT:])
+        load_x(X_PIECES[2])
         for quadrant in range(4):
             nc.sync.dma_start(
                 out=w_scales[32 * quadrant : 32 * quadrant + 16, :].bitcast(I32),
@@ -118,10 +119,12 @@ def tile_avey_pa_kernel(tc, x, g, W1_words, W1_scales, b1, out_0, out_1, out_2):
             )
         load_w(RIGHT, FEATURES)
         nc.sync.dma_start(out=bias_row[0:1, 0:LEFT], in_=b1.unsqueeze(0)[:, 0:LEFT])
-        load_x(X_PIECES[2])
-        load_w(0, HEAD)
-        load_w(LEFT, RIGHT)
         load_x(X_PIECES[3])
+        load_w(0, BANK)
+        load_x(X_PIECES[4])
+        load_w(BANK, HEAD)
+        load_w(LEFT, RIGHT)
+        load_x(X_PIECES[5])
 
 
         def sum_squares(i):
@@ -210,8 +213,8 @@ def tile_avey_pa_kernel(tc, x, g, W1_words, W1_scales, b1, out_0, out_1, out_2):
                 out=view, in0=view, scalar=0.0, in1=view, op0=ALU.max, op1=ALU.mult
             )
 
-        def store_head(i):
-            nc.sync.dma_start(out=head_rows[:, i, :], in_=wide[i][:, 0:HEAD])
+        def store_head(i, first, end):
+            nc.sync.dma_start(out=head_rows[:, i, first:end], in_=wide[i][:, first:end])
 
         def store_left(i):
             nc.sync.dma_start(out=left_rows[:, i, :], in_=wide[i][:, HEAD : HEAD + HALF])
@@ -279,10 +282,11 @@ def tile_avey_pa_kernel(tc, x, g, W1_words, W1_scales, b1, out_0, out_1, out_2):
         sum_squares(1)
         reciprocal_rms(1, 2)
         spread_bias(RIGHT, FEATURES)
+        sum_squares(2)
         nc.scalar.copy(out=bias[:, RIGHT:FEATURES], in_=spread[RIGHT][:])
+        reciprocal_rms(2, 3)
         quantise(0)
         normalise_rows(1)
-        sum_squares(2)
 
         right[0] = results.tile([P, HALF], F32, name="pre_right")
         wide[0] = results.tile([P, WIDE], F32, name="pre_wide")
@@ -293,11 +297,10 @@ def tile_avey_pa_kernel(tc, x, g, W1_words, W1_scales, b1, out_0, out_1, out_2):
         product(0, 0)
         product(0, BANK)
         add_bias(0, RIGHT)
-        nc.scalar.copy(out=bias[:, 0:BANK], in_=spread[0][:, 0:BANK])
-        reciprocal_rms(2, 3)
-        nc.scalar.copy(out=bias[:, BANK:HEAD], in_=spread[0][:, BANK:HEAD])
         sum_squares(3)
+        nc.scalar.copy(out=bias[:, 0:BANK], in_=spread[0][:, 0:BANK])
         reciprocal_rms(3, 4)
+        nc.scalar.copy(out=bias[:, BANK:HEAD], in_=spread[0][:, BANK:HEAD])
         relu(right[0][:])
         group(nc.vector.tensor_copy, 1)
         nc.vector.tensor_copy(out=bias[:, LEFT:RIGHT], in_=spread[LEFT][:])
@@ -319,15 +322,20 @@ def tile_avey_pa_kernel(tc, x, g, W1_words, W1_scales, b1, out_0, out_1, out_2):
                 j, start = waiting[0]
                 waiting.remove((j, start))
                 square(wide[j][:, start : start + BANK])
-                if start == BANK or (start == 0 and BANK in BY_VECTOR.get(j, ())):
-                    store_head(j)
                 if start == LEFT:
                     store_left(j)
+                elif j >= LAST - 1:
+                    store_head(j, start, start + BANK)
+                elif start == BANK:
+                    store_head(j, 0, HEAD)
 
         def finish_on_vector(i):
             for start in BY_VECTOR[i]:
                 squared_relu(wide[i][:, start : start + BANK])
-            store_left(i)
+                if start == LEFT:
+                    store_left(i)
+                else:
+                    store_head(i, start, start + BANK)
 
         for i in range(N_TILES):
             own = BY_VECTOR.get(i, ())
@@ -341,15 +349,19 @@ def tile_avey_pa_kernel(tc, x, g, W1_words, W1_scales, b1, out_0, out_1, out_2):
                 if i == LAST:
                     squared_relu(right[i][:])
                 product_plus_bias(i, BANK)
-                product_plus_bias(i, LEFT)
-                if i + 1 < N_TILES:
-                    quantise(i + 1)
+                if i == 1:
+                    quantise(2)
+                product(i, LEFT)
+                if i + 2 < N_TILES:
+                    flip(xn, i + 2)
+                    group(nc.scalar.copy, i + 2)
+                add_bias(i, LEFT)
+                if i + 2 < N_TILES:
+                    quantise(i + 2)
                 if 1 < i < LAST:
                     normalise_right(i - 2)
                 if i + 3 < N_TILES:
                     normalise_rows(i + 3)
-                if i + 2 < N_TILES:
-                    flip(xn, i + 2)
 
                 if i < LAST:
                     relu(right[i][:])
@@ -357,36 +369,36 @@ def tile_avey_pa_kernel(tc, x, g, W1_words, W1_scales, b1, out_0, out_1, out_2):
 
             if i == LAST - 1:
                 finish_on_vector(i)
-                normalise_right(i - 1)
 
             if i == 0:
                 sum_squares(4)
                 sum_squares(5)
-                group(nc.scalar.copy, 2)
-                reciprocal_rms(4, 6)
                 square(right[i][:])
+                reciprocal_rms(4, 6)
+                group(nc.scalar.copy, 2)
                 sum_squares(6)
-                sum_fourth(i)
                 sum_squares(7)
-                floor_sum(i)
                 reciprocal_rms(6, 8)
-                reciprocal_norm(i)
+            elif i < LAST:
+                sum_fourth(i - 1)
+                square_one_waiting()
+                floor_sum(i - 1)
+                square_one_waiting()
+                reciprocal_norm(i - 1)
+                square(right[i][:])
+                square_one_waiting()
             else:
+                sum_fourth(i - 1)
                 square_one_waiting()
-                if i < LAST:
-                    square(right[i][:])
-                if i + 2 < N_TILES:
-                    group(nc.scalar.copy, i + 2)
-                if i < LAST:
-                    square_one_waiting()
+                floor_sum(i - 1)
                 sum_fourth(i)
-                square_one_waiting()
+                reciprocal_norm(i - 1)
                 floor_sum(i)
-                square_one_waiting()
                 reciprocal_norm(i)
 
-            if i == LAST:
+            if i >= LAST - 1:
                 normalise_right(i - 1)
+            if i == LAST:
                 finish_on_vector(i)
             waiting.extend([(i, start) for start in rest])
 

@@ -84,8 +84,8 @@ def tile_avey_pa_kernel(tc, x, g, W1_words, W1_scales, b1, out_0, out_1, out_2):
 
         nc.vector.memset(eps_rms[:], EPS_RMS)
         nc.vector.memset(ones[:], 1.0)
-        nc.vector.memset(gain_row[:].bitcast(I32), 0)
         nc.vector.memset(bias_row[:, LEFT:].bitcast(I32), 0)
+        nc.vector.memset(gain_row[:].bitcast(I32), 0)
         nc.vector.memset(w_scales[:].bitcast(I32), 0)
         nc.vector.memset(floor[:], EPS_NORM * EPS_NORM)
         nc.vector.memset(neg_floor[:], -EPS_NORM * EPS_NORM)
@@ -106,9 +106,10 @@ def tile_avey_pa_kernel(tc, x, g, W1_words, W1_scales, b1, out_0, out_1, out_2):
 
         load_x(X_PIECES[0])
         nc.sync.dma_start(out=gain[:], in_=g.rearrange("(q t) -> q t", t=PACK))
-        nc.sync.dma_start(out=gain_row[0:1, :], in_=g.unsqueeze(0))
         load_x(X_PIECES[1])
         nc.sync.dma_start(out=bias_row[0:1, LEFT:], in_=b1.unsqueeze(0)[:, LEFT:])
+        nc.sync.dma_start(out=gain_row[0:1, :], in_=g.unsqueeze(0))
+        nc.sync.dma_start(out=bias_row[0:1, 0:LEFT], in_=b1.unsqueeze(0)[:, 0:LEFT])
         load_x(X_PIECES[2])
         for quadrant in range(4):
             nc.sync.dma_start(
@@ -118,7 +119,6 @@ def tile_avey_pa_kernel(tc, x, g, W1_words, W1_scales, b1, out_0, out_1, out_2):
                 .bitcast(I32),
             )
         load_w(RIGHT, FEATURES)
-        nc.sync.dma_start(out=bias_row[0:1, 0:LEFT], in_=b1.unsqueeze(0)[:, 0:LEFT])
         load_x(X_PIECES[3])
         load_w(0, BANK)
         load_x(X_PIECES[4])
@@ -267,12 +267,15 @@ def tile_avey_pa_kernel(tc, x, g, W1_words, W1_scales, b1, out_0, out_1, out_2):
         )
         sum_squares(0)
         reciprocal_rms(0, 1)
-        gain_spread = gain_bank.tile([P, K], F32, name="gain_spread")
-        nc.tensor.matmul(out=gain_spread[:], lhsT=ones[:], rhs=gain_row[:], start=True, stop=True)
+        spread_bias(RIGHT, FEATURES)
         rstd_spread = acc_banks.tile([P, P], F32, name="acc")
         nc.tensor.matmul(
             out=rstd_spread[:], lhsT=rstd[:, 0:1].to_broadcast([P, P]), rhs=identity[:], start=True, stop=True
         )
+        spread_bias(LEFT, RIGHT)
+        gain_spread = gain_bank.tile([P, K], F32, name="gain_spread")
+        nc.tensor.matmul(out=gain_spread[:], lhsT=ones[:], rhs=gain_row[:], start=True, stop=True)
+        spread_bias(0, LEFT)
         nc.vector.tensor_tensor(
             out=grouped[:, 0, :, :],
             in0=gained[:],
@@ -281,29 +284,26 @@ def tile_avey_pa_kernel(tc, x, g, W1_words, W1_scales, b1, out_0, out_1, out_2):
         )
         sum_squares(1)
         reciprocal_rms(1, 2)
-        spread_bias(RIGHT, FEATURES)
         sum_squares(2)
         nc.scalar.copy(out=bias[:, RIGHT:FEATURES], in_=spread[RIGHT][:])
         reciprocal_rms(2, 3)
         quantise(0)
         normalise_rows(1)
+        nc.vector.tensor_copy(out=bias[:, LEFT:RIGHT], in_=spread[LEFT][:])
 
         right[0] = results.tile([P, HALF], F32, name="pre_right")
         wide[0] = results.tile([P, WIDE], F32, name="pre_wide")
         product(0, RIGHT)
-        spread_bias(0, LEFT)
         flip(xn, 1)
-        spread_bias(LEFT, RIGHT)
         product(0, 0)
         product(0, BANK)
         add_bias(0, RIGHT)
-        sum_squares(3)
         nc.scalar.copy(out=bias[:, 0:BANK], in_=spread[0][:, 0:BANK])
-        reciprocal_rms(3, 4)
+        sum_squares(3)
         nc.scalar.copy(out=bias[:, BANK:HEAD], in_=spread[0][:, BANK:HEAD])
+        reciprocal_rms(3, 4)
         relu(right[0][:])
         group(nc.vector.tensor_copy, 1)
-        nc.vector.tensor_copy(out=bias[:, LEFT:RIGHT], in_=spread[LEFT][:])
         add_bias(0, 0)
         product(0, LEFT)
         normalise_rows(2)
@@ -354,7 +354,7 @@ def tile_avey_pa_kernel(tc, x, g, W1_words, W1_scales, b1, out_0, out_1, out_2):
                 product(i, LEFT)
                 if i + 2 < N_TILES:
                     flip(xn, i + 2)
-                    group(nc.scalar.copy, i + 2)
+                    group(nc.vector.tensor_copy if i + 2 in (5, 7) else nc.scalar.copy, i + 2)
                 add_bias(i, LEFT)
                 if i + 2 < N_TILES:
                     quantise(i + 2)

@@ -31,12 +31,12 @@ FLOPS = 2 * TOKENS * K * FEATURES
 LEFT = HEAD
 RIGHT = HEAD + HALF
 WIDE = HEAD + HALF
-WIDE_BANKS = (0, BANK, LEFT)
+WIDE_BANKS = (0, BANK)
 
 X_PIECES = ((0, 1), (1, 2), (2, 3), (3, 4), (4, 6), (6, 8))
 SCALED_AT_HEAD = 4
 WARM_UP = 10
-BY_VECTOR = {LAST - 1: (BANK, LEFT), LAST: (BANK, LEFT)}
+BY_VECTOR = {LAST - 1: (BANK,), LAST: (0, BANK)}
 
 
 def tile_avey_pa_kernel(tc, x, g, W1_words, W1_scales, b1, out_0, out_1, out_2):
@@ -56,7 +56,9 @@ def tile_avey_pa_kernel(tc, x, g, W1_words, W1_scales, b1, out_0, out_1, out_2):
         results = stack.enter_context(tc.tile_pool(name="results", bufs=N_TILES))
         gain_bank = stack.enter_context(tc.psum_pool(name="gain_bank", bufs=1))
         flip_banks = stack.enter_context(tc.psum_pool(name="flip_banks", bufs=1))
-        acc_banks = stack.enter_context(tc.psum_pool(name="acc_banks", bufs=6))
+        acc_banks = stack.enter_context(tc.psum_pool(name="acc_banks", bufs=5))
+        back_bank = stack.enter_context(tc.psum_pool(name="back_bank", bufs=1))
+        clipped_tiles = stack.enter_context(tc.tile_pool(name="clipped_tiles", bufs=2))
 
         x_sb = keep.tile([P, N_TILES, K], BF16)
         xn = keep.tile([P, N_TILES, K], BF16)
@@ -64,6 +66,7 @@ def tile_avey_pa_kernel(tc, x, g, W1_words, W1_scales, b1, out_0, out_1, out_2):
         grouped = keep.tile([P, N_TILES, P, PACK], BF16, align_bytes=64)
         gain = keep.tile([P, PACK], BF16)
         bias = keep.tile([P, FEATURES], BF16)
+        bias_left = keep.tile([P, PACK], F32)
         bias_row = keep.tile([P, FEATURES], BF16)
         gain_row = keep.tile([P, K], BF16)
         ones = keep.tile([P, P], BF16)
@@ -175,6 +178,7 @@ def tile_avey_pa_kernel(tc, x, g, W1_words, W1_scales, b1, out_0, out_1, out_2):
 
         right = {}
         wide = {}
+        left = {}
         acc = {}
 
         def product(i, start):
@@ -200,6 +204,45 @@ def tile_avey_pa_kernel(tc, x, g, W1_words, W1_scales, b1, out_0, out_1, out_2):
             product(i, start)
             add_bias(i, start)
 
+        clipped = {}
+        back = {}
+
+        def left_product(i):
+            acc[(i, LEFT)] = acc_banks.tile([P, 4, P], F32, name="acc")
+            for c in range(4):
+                cols = slice(LEFT + c * P, LEFT + (c + 1) * P)
+                nc.tensor.matmul_mx(
+                    out=acc[(i, LEFT)][:, c, :],
+                    lhsT=w_codes[:, cols].bitcast(FP8X4),
+                    lhsT_scale=w_scales[PACK * (LEFT // BANK) :, c * P : (c + 1) * P],
+                    rhs=xq_codes[:, i, :].bitcast(FP8X4),
+                    rhs_scale=xq_scales[:, i, :],
+                    start=True,
+                    stop=True,
+                )
+
+        def left_bias_relu(i):
+            clipped[i] = clipped_tiles.tile([P, 4, P], F32, name="clipped_left")
+            for c in (3, 2, 1, 0):
+                nc.vector.tensor_scalar(
+                    out=clipped[i][:, c, :],
+                    in0=acc[(i, LEFT)][:, c, :],
+                    scalar1=bias_left[:, c : c + 1],
+                    scalar2=0.0,
+                    op0=ALU.add,
+                    op1=ALU.max,
+                )
+
+        def left_back(i):
+            back[i] = back_bank.tile([P, 4, P], F32, name="back")
+            for c in range(4):
+                nc.tensor.transpose(back[i][:, c, :], clipped[i][:, c, :], identity[:])
+
+        def left_square(i):
+            left[i] = results.tile([P, HALF], F32, name="left_results")
+            nc.scalar.activation(out=left[i][:], in_=back[i][:].rearrange("p c f -> p (c f)"), func=ACT.Square)
+            nc.sync.dma_start(out=left_rows[:, i, :], in_=left[i][:])
+
         def relu(view):
             nc.gpsimd.tensor_scalar(
                 out=view, in0=view, scalar1=FLT_BIG, scalar2=0.0, op0=ALU.min, op1=ALU.max
@@ -215,9 +258,6 @@ def tile_avey_pa_kernel(tc, x, g, W1_words, W1_scales, b1, out_0, out_1, out_2):
 
         def store_head(i, first, end):
             nc.sync.dma_start(out=head_rows[:, i, first:end], in_=wide[i][:, first:end])
-
-        def store_left(i):
-            nc.sync.dma_start(out=left_rows[:, i, :], in_=wide[i][:, HEAD : HEAD + HALF])
 
         def sum_fourth(i):
             fourth = work.tile([P, HALF], F32)
@@ -237,6 +277,17 @@ def tile_avey_pa_kernel(tc, x, g, W1_words, W1_scales, b1, out_0, out_1, out_2):
                 func=ACT.Abs_reciprocal_sqrt,
                 bias=floor[:],
             )
+
+        def normalise_right_on_gpsimd(i):
+            nc.gpsimd.tensor_scalar(
+                out=right[i][:],
+                in0=right[i][:],
+                scalar1=right_inv[:, i : i + 1],
+                scalar2=1.0,
+                op0=ALU.mult,
+                op1=ALU.mult,
+            )
+            nc.sync.dma_start(out=right_rows[:, i, :], in_=right[i][:])
 
         def normalise_right(i):
             nc.vector.tensor_scalar_mul(out=right[i][:], in0=right[i][:], scalar1=right_inv[:, i : i + 1])
@@ -272,7 +323,15 @@ def tile_avey_pa_kernel(tc, x, g, W1_words, W1_scales, b1, out_0, out_1, out_2):
         nc.tensor.matmul(
             out=rstd_spread[:], lhsT=rstd[:, 0:1].to_broadcast([P, P]), rhs=identity[:], start=True, stop=True
         )
-        spread_bias(LEFT, RIGHT)
+        left_turned = acc_banks.tile([P, PACK], F32, name="acc")
+        for c in range(4):
+            nc.tensor.matmul(
+                out=left_turned[:, c : c + 1],
+                lhsT=bias_row[:, LEFT + c * P : LEFT + (c + 1) * P],
+                rhs=ones[:, 0:1],
+                start=True,
+                stop=True,
+            )
         gain_spread = gain_bank.tile([P, K], F32, name="gain_spread")
         nc.tensor.matmul(out=gain_spread[:], lhsT=ones[:], rhs=gain_row[:], start=True, stop=True)
         spread_bias(0, LEFT)
@@ -289,10 +348,10 @@ def tile_avey_pa_kernel(tc, x, g, W1_words, W1_scales, b1, out_0, out_1, out_2):
         reciprocal_rms(2, 3)
         quantise(0)
         normalise_rows(1)
-        nc.vector.tensor_copy(out=bias[:, LEFT:RIGHT], in_=spread[LEFT][:])
+        nc.vector.tensor_copy(out=bias_left[:], in_=left_turned[:])
 
         right[0] = results.tile([P, HALF], F32, name="pre_right")
-        wide[0] = results.tile([P, WIDE], F32, name="pre_wide")
+        wide[0] = results.tile([P, HEAD], F32, name="pre_wide")
         product(0, RIGHT)
         flip(xn, 1)
         product(0, 0)
@@ -305,14 +364,16 @@ def tile_avey_pa_kernel(tc, x, g, W1_words, W1_scales, b1, out_0, out_1, out_2):
         relu(right[0][:])
         group(nc.vector.tensor_copy, 1)
         add_bias(0, 0)
-        product(0, LEFT)
+        left_product(0)
         normalise_rows(2)
         flip(xn, 2)
         add_bias(0, BANK)
-        quantise(1)
-        add_bias(0, LEFT)
         relu(wide[0][:])
+        quantise(1)
+        left_bias_relu(0)
         normalise_rows(3)
+        product(1, RIGHT)
+        left_back(0)
 
 
         waiting = []
@@ -322,9 +383,7 @@ def tile_avey_pa_kernel(tc, x, g, W1_words, W1_scales, b1, out_0, out_1, out_2):
                 j, start = waiting[0]
                 waiting.remove((j, start))
                 square(wide[j][:, start : start + BANK])
-                if start == LEFT:
-                    store_left(j)
-                elif j >= LAST - 1:
+                if j >= LAST - 1:
                     store_head(j, start, start + BANK)
                 elif start == BANK:
                     store_head(j, 0, HEAD)
@@ -332,40 +391,42 @@ def tile_avey_pa_kernel(tc, x, g, W1_words, W1_scales, b1, out_0, out_1, out_2):
         def finish_on_vector(i):
             for start in BY_VECTOR[i]:
                 squared_relu(wide[i][:, start : start + BANK])
-                if start == LEFT:
-                    store_left(i)
-                else:
-                    store_head(i, start, start + BANK)
+                store_head(i, start, start + BANK)
 
         for i in range(N_TILES):
             own = BY_VECTOR.get(i, ())
             rest = [start for start in WIDE_BANKS if start not in own]
             if i > 0:
                 right[i] = results.tile([P, HALF], F32, name="pre_right")
-                wide[i] = results.tile([P, WIDE], F32, name="pre_wide")
+                wide[i] = results.tile([P, HEAD], F32, name="pre_wide")
 
-                product_plus_bias(i, RIGHT)
-                product_plus_bias(i, 0)
+                if i > 1:
+                    product(i, RIGHT)
+                add_bias(i, RIGHT)
+                left_product(i)
+                left_bias_relu(i)
                 if i == LAST:
                     squared_relu(right[i][:])
-                product_plus_bias(i, BANK)
+                product_plus_bias(i, 0)
                 if i == 1:
                     quantise(2)
-                product(i, LEFT)
+                product(i, BANK)
                 if i + 2 < N_TILES:
                     flip(xn, i + 2)
-                    group(nc.vector.tensor_copy if i + 2 in (5, 7) else nc.scalar.copy, i + 2)
-                add_bias(i, LEFT)
+                    group(nc.vector.tensor_copy if i + 2 in (4, 5, 6, 7) else nc.scalar.copy, i + 2)
+                left_back(i)
+                add_bias(i, BANK)
                 if i + 2 < N_TILES:
                     quantise(i + 2)
-                if 1 < i < LAST:
-                    normalise_right(i - 2)
                 if i + 3 < N_TILES:
                     normalise_rows(i + 3)
 
                 if i < LAST:
                     relu(right[i][:])
-                relu(wide[i][:, rest[0] : rest[-1] + BANK])
+                if 1 < i < LAST:
+                    normalise_right_on_gpsimd(i - 2)
+                if rest:
+                    relu(wide[i][:, rest[0] : rest[-1] + BANK])
 
             if i == LAST - 1:
                 finish_on_vector(i)
@@ -376,6 +437,7 @@ def tile_avey_pa_kernel(tc, x, g, W1_words, W1_scales, b1, out_0, out_1, out_2):
                 square(right[i][:])
                 reciprocal_rms(4, 6)
                 group(nc.scalar.copy, 2)
+                left_square(0)
                 sum_squares(6)
                 sum_squares(7)
                 reciprocal_rms(6, 8)
@@ -386,13 +448,14 @@ def tile_avey_pa_kernel(tc, x, g, W1_words, W1_scales, b1, out_0, out_1, out_2):
                 square_one_waiting()
                 reciprocal_norm(i - 1)
                 square(right[i][:])
-                square_one_waiting()
+                left_square(i)
             else:
                 sum_fourth(i - 1)
                 square_one_waiting()
                 floor_sum(i - 1)
                 sum_fourth(i)
                 reciprocal_norm(i - 1)
+                left_square(i)
                 floor_sum(i)
                 reciprocal_norm(i)
 

@@ -35,7 +35,7 @@ WIDE_BANKS = (0, BANK)
 
 X_PIECES = ((0, 1), (1, 2), (2, 3), (3, 4), (4, 6), (6, 8))
 SCALED_AT_HEAD = 4
-WARM_UP = 10
+WARM_UP = 12
 BY_VECTOR = {LAST - 1: (BANK,), LAST: (0, BANK)}
 
 
@@ -53,11 +53,12 @@ def tile_avey_pa_kernel(tc, x, g, W1_words, W1_scales, b1, out_0, out_1, out_2):
         stack.enter_context(tc.manual_schedule())
         keep = stack.enter_context(tc.tile_pool(name="keep", bufs=1))
         work = stack.enter_context(tc.tile_pool(name="work", bufs=3))
-        results = stack.enter_context(tc.tile_pool(name="results", bufs=N_TILES))
+        heads_pool = stack.enter_context(tc.tile_pool(name="heads_pool", bufs=N_TILES))
+        results = stack.enter_context(tc.tile_pool(name="results", bufs=2 * N_TILES))
         gain_bank = stack.enter_context(tc.psum_pool(name="gain_bank", bufs=1))
         flip_banks = stack.enter_context(tc.psum_pool(name="flip_banks", bufs=1))
-        acc_banks = stack.enter_context(tc.psum_pool(name="acc_banks", bufs=5))
-        back_bank = stack.enter_context(tc.psum_pool(name="back_bank", bufs=1))
+        acc_banks = stack.enter_context(tc.psum_pool(name="acc_banks", bufs=4))
+        back_bank = stack.enter_context(tc.psum_pool(name="back_bank", bufs=2))
         clipped_tiles = stack.enter_context(tc.tile_pool(name="clipped_tiles", bufs=2))
 
         x_sb = keep.tile([P, N_TILES, K], BF16)
@@ -65,8 +66,8 @@ def tile_avey_pa_kernel(tc, x, g, W1_words, W1_scales, b1, out_0, out_1, out_2):
         gained = keep.tile([P, P, PACK], F32)
         grouped = keep.tile([P, N_TILES, P, PACK], BF16, align_bytes=64)
         gain = keep.tile([P, PACK], BF16)
-        bias = keep.tile([P, FEATURES], BF16)
-        bias_left = keep.tile([P, PACK], F32)
+        bias = keep.tile([P, HEAD], BF16)
+        bias_sides = keep.tile([P, 8], F32)
         bias_row = keep.tile([P, FEATURES], BF16)
         gain_row = keep.tile([P, K], BF16)
         ones = keep.tile([P, P], BF16)
@@ -87,14 +88,14 @@ def tile_avey_pa_kernel(tc, x, g, W1_words, W1_scales, b1, out_0, out_1, out_2):
 
         nc.vector.memset(eps_rms[:], EPS_RMS)
         nc.vector.memset(ones[:], 1.0)
-        nc.vector.memset(bias_row[:, LEFT:].bitcast(I32), 0)
         nc.vector.memset(gain_row[:].bitcast(I32), 0)
+        nc.vector.memset(bias_row[:, 0:LEFT].bitcast(I32), 0)
         nc.vector.memset(w_scales[:].bitcast(I32), 0)
         nc.vector.memset(floor[:], EPS_NORM * EPS_NORM)
         nc.vector.memset(neg_floor[:], -EPS_NORM * EPS_NORM)
         nc.scalar.activation(out=table_warm[:], in_=eps_rms[:], func=ACT.Abs_reciprocal_sqrt)
         make_identity(nc, identity[:])
-        nc.gpsimd.memset(bias_row[:, 0:LEFT].bitcast(F32), 0.0)
+        nc.gpsimd.memset(bias_row[:, LEFT:].bitcast(F32), 0.0)
 
 
         def load_x(piece):
@@ -109,10 +110,10 @@ def tile_avey_pa_kernel(tc, x, g, W1_words, W1_scales, b1, out_0, out_1, out_2):
 
         load_x(X_PIECES[0])
         nc.sync.dma_start(out=gain[:], in_=g.rearrange("(q t) -> q t", t=PACK))
-        load_x(X_PIECES[1])
-        nc.sync.dma_start(out=bias_row[0:1, LEFT:], in_=b1.unsqueeze(0)[:, LEFT:])
         nc.sync.dma_start(out=gain_row[0:1, :], in_=g.unsqueeze(0))
+        load_x(X_PIECES[1])
         nc.sync.dma_start(out=bias_row[0:1, 0:LEFT], in_=b1.unsqueeze(0)[:, 0:LEFT])
+        nc.sync.dma_start(out=bias_row[0:1, LEFT:], in_=b1.unsqueeze(0)[:, LEFT:])
         load_x(X_PIECES[2])
         for quadrant in range(4):
             nc.sync.dma_start(
@@ -121,11 +122,11 @@ def tile_avey_pa_kernel(tc, x, g, W1_words, W1_scales, b1, out_0, out_1, out_2):
                 .rearrange("r (j n) -> j r n", n=BANK)
                 .bitcast(I32),
             )
-        load_w(RIGHT, FEATURES)
-        load_x(X_PIECES[3])
         load_w(0, BANK)
-        load_x(X_PIECES[4])
+        load_x(X_PIECES[3])
         load_w(BANK, HEAD)
+        load_x(X_PIECES[4])
+        load_w(RIGHT, FEATURES)
         load_w(LEFT, RIGHT)
         load_x(X_PIECES[5])
 
@@ -195,7 +196,7 @@ def tile_avey_pa_kernel(tc, x, g, W1_words, W1_scales, b1, out_0, out_1, out_2):
             )
 
         def add_bias(i, start):
-            target = right[i][:, 0:BANK] if start == RIGHT else wide[i][:, start : start + BANK]
+            target = wide[i][:, start : start + BANK]
             nc.vector.tensor_tensor(
                 out=target, in0=acc[(i, start)][:], in1=bias[:, start : start + BANK], op=ALU.add
             )
@@ -207,40 +208,46 @@ def tile_avey_pa_kernel(tc, x, g, W1_words, W1_scales, b1, out_0, out_1, out_2):
         clipped = {}
         back = {}
 
-        def left_product(i):
-            acc[(i, LEFT)] = acc_banks.tile([P, 4, P], F32, name="acc")
+        def side_product(i, side):
+            acc[(i, side)] = acc_banks.tile([P, 4, P], F32, name="acc")
             for c in range(4):
-                cols = slice(LEFT + c * P, LEFT + (c + 1) * P)
+                cols = slice(side + c * P, side + (c + 1) * P)
                 nc.tensor.matmul_mx(
-                    out=acc[(i, LEFT)][:, c, :],
+                    out=acc[(i, side)][:, c, :],
                     lhsT=w_codes[:, cols].bitcast(FP8X4),
-                    lhsT_scale=w_scales[PACK * (LEFT // BANK) :, c * P : (c + 1) * P],
+                    lhsT_scale=w_scales[PACK * (side // BANK) :, c * P : (c + 1) * P],
                     rhs=xq_codes[:, i, :].bitcast(FP8X4),
                     rhs_scale=xq_scales[:, i, :],
                     start=True,
                     stop=True,
                 )
 
-        def left_bias_relu(i):
-            clipped[i] = clipped_tiles.tile([P, 4, P], F32, name="clipped_left")
+        def side_bias_relu(i, side):
+            clipped[(i, side)] = clipped_tiles.tile([P, 4, P], F32, name="clipped_side")
             for c in (3, 2, 1, 0):
+                column = (side - LEFT) // P + c
                 nc.vector.tensor_scalar(
-                    out=clipped[i][:, c, :],
-                    in0=acc[(i, LEFT)][:, c, :],
-                    scalar1=bias_left[:, c : c + 1],
+                    out=clipped[(i, side)][:, c, :],
+                    in0=acc[(i, side)][:, c, :],
+                    scalar1=bias_sides[:, column : column + 1],
                     scalar2=0.0,
                     op0=ALU.add,
                     op1=ALU.max,
                 )
 
-        def left_back(i):
-            back[i] = back_bank.tile([P, 4, P], F32, name="back")
+        def side_back(i, side):
+            back[(i, side)] = back_bank.tile([P, 4, P], F32, name="back")
             for c in range(4):
-                nc.tensor.transpose(back[i][:, c, :], clipped[i][:, c, :], identity[:])
+                nc.tensor.transpose(back[(i, side)][:, c, :], clipped[(i, side)][:, c, :], identity[:])
 
-        def left_square(i):
-            left[i] = results.tile([P, HALF], F32, name="left_results")
-            nc.scalar.activation(out=left[i][:], in_=back[i][:].rearrange("p c f -> p (c f)"), func=ACT.Square)
+        def side_square(i, side):
+            target = right if side == RIGHT else left
+            target[i] = results.tile([P, HALF], F32, name="side_results")
+            nc.scalar.activation(
+                out=target[i][:], in_=back[(i, side)][:].rearrange("p c f -> p (c f)"), func=ACT.Square
+            )
+
+        def store_left(i):
             nc.sync.dma_start(out=left_rows[:, i, :], in_=left[i][:])
 
         def relu(view):
@@ -287,10 +294,11 @@ def tile_avey_pa_kernel(tc, x, g, W1_words, W1_scales, b1, out_0, out_1, out_2):
                 op0=ALU.mult,
                 op1=ALU.mult,
             )
-            nc.sync.dma_start(out=right_rows[:, i, :], in_=right[i][:])
 
         def normalise_right(i):
             nc.vector.tensor_scalar_mul(out=right[i][:], in0=right[i][:], scalar1=right_inv[:, i : i + 1])
+
+        def store_right(i):
             nc.sync.dma_start(out=right_rows[:, i, :], in_=right[i][:])
 
         spread = {}
@@ -318,23 +326,22 @@ def tile_avey_pa_kernel(tc, x, g, W1_words, W1_scales, b1, out_0, out_1, out_2):
         )
         sum_squares(0)
         reciprocal_rms(0, 1)
-        spread_bias(RIGHT, FEATURES)
+        gain_spread = gain_bank.tile([P, K], F32, name="gain_spread")
+        nc.tensor.matmul(out=gain_spread[:], lhsT=ones[:], rhs=gain_row[:], start=True, stop=True)
         rstd_spread = acc_banks.tile([P, P], F32, name="acc")
         nc.tensor.matmul(
             out=rstd_spread[:], lhsT=rstd[:, 0:1].to_broadcast([P, P]), rhs=identity[:], start=True, stop=True
         )
-        left_turned = acc_banks.tile([P, PACK], F32, name="acc")
-        for c in range(4):
+        spread_bias(0, LEFT)
+        sides_turned = acc_banks.tile([P, 8], F32, name="acc")
+        for c in range(8):
             nc.tensor.matmul(
-                out=left_turned[:, c : c + 1],
+                out=sides_turned[:, c : c + 1],
                 lhsT=bias_row[:, LEFT + c * P : LEFT + (c + 1) * P],
                 rhs=ones[:, 0:1],
                 start=True,
                 stop=True,
             )
-        gain_spread = gain_bank.tile([P, K], F32, name="gain_spread")
-        nc.tensor.matmul(out=gain_spread[:], lhsT=ones[:], rhs=gain_row[:], start=True, stop=True)
-        spread_bias(0, LEFT)
         nc.vector.tensor_tensor(
             out=grouped[:, 0, :, :],
             in0=gained[:],
@@ -343,128 +350,120 @@ def tile_avey_pa_kernel(tc, x, g, W1_words, W1_scales, b1, out_0, out_1, out_2):
         )
         sum_squares(1)
         reciprocal_rms(1, 2)
+        nc.scalar.copy(out=bias[:, 0:BANK], in_=spread[0][:, 0:BANK])
         sum_squares(2)
-        nc.scalar.copy(out=bias[:, RIGHT:FEATURES], in_=spread[RIGHT][:])
+        nc.scalar.copy(out=bias[:, BANK:HEAD], in_=spread[0][:, BANK:HEAD])
         reciprocal_rms(2, 3)
+        sum_squares(3)
+        sum_squares(4)
+        reciprocal_rms(3, 5)
+        sum_squares(5)
+        sum_squares(6)
+        sum_squares(7)
+        reciprocal_rms(5, 8)
         quantise(0)
         normalise_rows(1)
-        nc.vector.tensor_copy(out=bias_left[:], in_=left_turned[:])
+        nc.vector.tensor_copy(out=bias_sides[:], in_=sides_turned[:])
 
-        right[0] = results.tile([P, HALF], F32, name="pre_right")
-        wide[0] = results.tile([P, HEAD], F32, name="pre_wide")
-        product(0, RIGHT)
-        flip(xn, 1)
+        wide[0] = heads_pool.tile([P, HEAD], F32, name="pre_wide")
         product(0, 0)
+        flip(xn, 1)
         product(0, BANK)
-        add_bias(0, RIGHT)
-        nc.scalar.copy(out=bias[:, 0:BANK], in_=spread[0][:, 0:BANK])
-        sum_squares(3)
-        nc.scalar.copy(out=bias[:, BANK:HEAD], in_=spread[0][:, BANK:HEAD])
-        reciprocal_rms(3, 4)
-        relu(right[0][:])
-        group(nc.vector.tensor_copy, 1)
         add_bias(0, 0)
-        left_product(0)
-        normalise_rows(2)
-        flip(xn, 2)
+        group(nc.vector.tensor_copy, 1)
         add_bias(0, BANK)
         relu(wide[0][:])
         quantise(1)
-        left_bias_relu(0)
-        normalise_rows(3)
-        product(1, RIGHT)
-        left_back(0)
+        side_product(0, RIGHT)
+        side_product(0, LEFT)
+        product(1, 0)
+        product(1, BANK)
+        normalise_rows(2)
+        flip(xn, 2)
+        side_bias_relu(0, RIGHT)
+        side_back(0, RIGHT)
+        side_bias_relu(0, LEFT)
+        group(nc.vector.tensor_copy, 2)
+        side_back(0, LEFT)
+        square(wide[0][:])
+        store_head(0, 0, HEAD)
+        side_square(0, RIGHT)
+        side_square(0, LEFT)
+        store_left(0)
+        sum_fourth(0)
 
-
-        waiting = []
-
-        def square_one_waiting():
-            if waiting:
-                j, start = waiting[0]
-                waiting.remove((j, start))
-                square(wide[j][:, start : start + BANK])
-                if j >= LAST - 1:
-                    store_head(j, start, start + BANK)
-                elif start == BANK:
-                    store_head(j, 0, HEAD)
-
-        def finish_on_vector(i):
-            for start in BY_VECTOR[i]:
-                squared_relu(wide[i][:, start : start + BANK])
-                store_head(i, start, start + BANK)
-
-        for i in range(N_TILES):
-            own = BY_VECTOR.get(i, ())
-            rest = [start for start in WIDE_BANKS if start not in own]
-            if i > 0:
-                right[i] = results.tile([P, HALF], F32, name="pre_right")
-                wide[i] = results.tile([P, HEAD], F32, name="pre_wide")
-
-                if i > 1:
-                    product(i, RIGHT)
-                add_bias(i, RIGHT)
-                left_product(i)
-                left_bias_relu(i)
-                if i == LAST:
-                    squared_relu(right[i][:])
-                product_plus_bias(i, 0)
-                if i == 1:
-                    quantise(2)
-                product(i, BANK)
-                if i + 2 < N_TILES:
-                    flip(xn, i + 2)
-                    group(nc.vector.tensor_copy if i + 2 in (4, 5, 6, 7) else nc.scalar.copy, i + 2)
-                left_back(i)
+        for i in range(1, N_TILES):
+            wide[i] = heads_pool.tile([P, HEAD], F32, name="pre_wide")
+            if i < LAST:
+                add_bias(i, 0)
                 add_bias(i, BANK)
-                if i + 2 < N_TILES:
-                    quantise(i + 2)
-                if i + 3 < N_TILES:
-                    normalise_rows(i + 3)
-
-                if i < LAST:
-                    relu(right[i][:])
-                if 1 < i < LAST:
+                quantise(i + 1)
+                side_product(i, RIGHT)
+                side_product(i, LEFT)
+            if i < LAST - 1:
+                relu(wide[i][:])
+                if i > 1:
                     normalise_right_on_gpsimd(i - 2)
-                if rest:
-                    relu(wide[i][:, rest[0] : rest[-1] + BANK])
-
-            if i == LAST - 1:
-                finish_on_vector(i)
-
-            if i == 0:
-                sum_squares(4)
-                sum_squares(5)
-                square(right[i][:])
-                reciprocal_rms(4, 6)
-                group(nc.scalar.copy, 2)
-                left_square(0)
-                sum_squares(6)
-                sum_squares(7)
-                reciprocal_rms(6, 8)
-            elif i < LAST:
-                sum_fourth(i - 1)
-                square_one_waiting()
-                floor_sum(i - 1)
-                square_one_waiting()
-                reciprocal_norm(i - 1)
-                square(right[i][:])
-                left_square(i)
+            if i < LAST - 1:
+                product(i + 1, 0)
+                product(i + 1, BANK)
+            elif i == LAST - 1:
+                side_product(LAST, RIGHT)
+                side_product(LAST, LEFT)
             else:
-                sum_fourth(i - 1)
-                square_one_waiting()
+                product(i, 0)
+                product(i, BANK)
+            if i + 2 < N_TILES:
+                normalise_rows(i + 2)
+                flip(xn, i + 2)
+            side_bias_relu(i, RIGHT)
+            side_back(i, RIGHT)
+            side_bias_relu(i, LEFT)
+            if i + 2 < N_TILES:
+                group(nc.vector.tensor_copy, i + 2)
+            side_back(i, LEFT)
+            if i < LAST - 1:
+                square(wide[i][:])
+                store_head(i, 0, HEAD)
                 floor_sum(i - 1)
-                sum_fourth(i)
+                side_square(i, RIGHT)
                 reciprocal_norm(i - 1)
-                left_square(i)
+                if i > 1:
+                    store_right(i - 2)
+                side_square(i, LEFT)
+                store_left(i)
+                sum_fourth(i)
+            elif i == LAST - 1:
+                floor_sum(i - 1)
+                side_square(i, RIGHT)
+                reciprocal_norm(i - 1)
+                side_square(i, LEFT)
+                normalise_right(i - 2)
+                store_right(i - 2)
+                store_left(i)
+                sum_fourth(i)
+            else:
+                squared_relu(wide[i - 1][:, 0:BANK])
+                store_head(i - 1, 0, BANK)
+                normalise_right(i - 2)
+                store_right(i - 2)
+                squared_relu(wide[i - 1][:, BANK:HEAD])
+                store_head(i - 1, BANK, HEAD)
+                add_bias(i, 0)
+                add_bias(i, BANK)
+                side_square(i, RIGHT)
+                floor_sum(i - 1)
+                side_square(i, LEFT)
+                reciprocal_norm(i - 1)
+                sum_fourth(i)
+                store_left(i)
+                squared_relu(wide[i][:, 0:BANK])
+                store_head(i, 0, BANK)
+                normalise_right(i - 1)
+                store_right(i - 1)
+                squared_relu(wide[i][:, BANK:HEAD])
+                store_head(i, BANK, HEAD)
                 floor_sum(i)
                 reciprocal_norm(i)
-
-            if i >= LAST - 1:
-                normalise_right(i - 1)
-            if i == LAST:
-                finish_on_vector(i)
-            waiting.extend([(i, start) for start in rest])
-
-        for start in WIDE_BANKS:
-            square_one_waiting()
-        normalise_right(LAST)
+                normalise_right(i)
+                store_right(i)

@@ -137,6 +137,18 @@ def tile_avey_pa_kernel(tc, x, g, W1_words, W1_scales, b1, out_0, out_1, out_2):
                 out=squares[:], in_=x_sb[:, i, :], func=ACT.Square, accum_out=sum_sq[:, i : i + 1]
             )
 
+        def sum_squares_on_vector(i):
+            squares = work.tile([P, K], BF16)
+            nc.vector.scalar_tensor_tensor(
+                out=squares[:],
+                in0=x_sb[:, i, :],
+                scalar=1.0,
+                in1=x_sb[:, i, :],
+                op0=ALU.mult,
+                op1=ALU.mult,
+                accum_out=sum_sq[:, i : i + 1],
+            )
+
         def reciprocal_rms(first, end):
             nc.scalar.activation(
                 out=rstd[:, first:end],
@@ -342,18 +354,17 @@ def tile_avey_pa_kernel(tc, x, g, W1_words, W1_scales, b1, out_0, out_1, out_2):
                 start=True,
                 stop=True,
             )
+        sum_squares_on_vector(1)
         nc.vector.tensor_tensor(
             out=grouped[:, 0, :, :],
             in0=gained[:],
             in1=rstd_spread[:].unsqueeze(2).to_broadcast([P, P, PACK]),
             op=ALU.mult,
         )
-        sum_squares(1)
-        reciprocal_rms(1, 2)
-        nc.scalar.copy(out=bias[:, 0:BANK], in_=spread[0][:, 0:BANK])
         sum_squares(2)
+        reciprocal_rms(1, 3)
+        nc.scalar.copy(out=bias[:, 0:BANK], in_=spread[0][:, 0:BANK])
         nc.scalar.copy(out=bias[:, BANK:HEAD], in_=spread[0][:, BANK:HEAD])
-        reciprocal_rms(2, 3)
         sum_squares(3)
         sum_squares(4)
         reciprocal_rms(3, 5)
@@ -420,16 +431,16 @@ def tile_avey_pa_kernel(tc, x, g, W1_words, W1_scales, b1, out_0, out_1, out_2):
             side_back(i, RIGHT)
             side_bias_relu(i, LEFT)
             if i + 2 < N_TILES:
-                group(nc.vector.tensor_copy, i + 2)
+                group(nc.scalar.copy if i + 2 in (4, 5, 6) else nc.vector.tensor_copy, i + 2)
             side_back(i, LEFT)
             if i < LAST - 1:
+                if i > 1:
+                    store_right(i - 2)
                 square(wide[i][:])
                 store_head(i, 0, HEAD)
                 floor_sum(i - 1)
                 side_square(i, RIGHT)
                 reciprocal_norm(i - 1)
-                if i > 1:
-                    store_right(i - 2)
                 side_square(i, LEFT)
                 store_left(i)
                 sum_fourth(i)

from contextlib import ExitStack

import concourse.mybir as mybir
from concourse.masks import make_identity

F32 = mybir.dt.float32
BF16 = mybir.dt.bfloat16
I32 = mybir.dt.int32
U32 = mybir.dt.uint32
U8 = mybir.dt.uint8
FP8X4 = mybir.dt.float8_e4m3fn_x4
ACT = mybir.ActivationFunctionType
ALU = mybir.AluOpType

P = 128
PACK = 4
TOKENS = 1024
K = P * PACK
HEAD = 1024
HALF = 512
FEATURES = HEAD + 2 * HALF
BANK = 512
N_TILES = TOKENS // P
LAST = N_TILES - 1
EPS_RMS = 1e-6
EPS_NORM = 1e-12
FLT_BIG = 3.0e38

FLOPS = 2 * TOKENS * K * FEATURES

LEFT = HEAD
RIGHT = HEAD + HALF
WIDE = HEAD + HALF
WIDE_BANKS = (0, BANK)

X_PIECES = ((0, 1), (1, 2), (2, 3), (3, 4), (4, 6), (6, 8))
SCALED_AT_HEAD = 4
WARM_UP = 12
BY_VECTOR = {LAST - 1: (BANK,), LAST: (0, BANK)}


def tile_avey_pa_kernel(tc, x, g, W1_words, W1_scales, b1, out_0, out_1, out_2):
    nc = tc.nc

    x_rows = x.flatten_outer_dims().rearrange("(p i) k -> p i k", i=N_TILES)
    right_rows = out_2.flatten_outer_dims().rearrange("(p i) n -> p i n", i=N_TILES)
    head_rows = out_0.flatten_outer_dims().rearrange("(p i) n -> p i n", i=N_TILES)
    left_rows = out_1.flatten_outer_dims().rearrange("(p i) n -> p i n", i=N_TILES)
    w_bytes = W1_words.rearrange("o p n t -> p (o n t)")
    w_scale_rows = W1_scales.rearrange("o q n -> (o q) n")

    with ExitStack() as stack:
        stack.enter_context(tc.manual_schedule())
        keep = stack.enter_context(tc.tile_pool(name="keep", bufs=1))
        work = stack.enter_context(tc.tile_pool(name="work", bufs=3))
        heads_pool = stack.enter_context(tc.tile_pool(name="heads_pool", bufs=N_TILES))
        results = stack.enter_context(tc.tile_pool(name="results", bufs=2 * N_TILES))
        gain_bank = stack.enter_context(tc.psum_pool(name="gain_bank", bufs=1))
        flip_banks = stack.enter_context(tc.psum_pool(name="flip_banks", bufs=1))
        acc_banks = stack.enter_context(tc.psum_pool(name="acc_banks", bufs=4))
        back_bank = stack.enter_context(tc.psum_pool(name="back_bank", bufs=2))
        clipped_tiles = stack.enter_context(tc.tile_pool(name="clipped_tiles", bufs=2))

        x_sb = keep.tile([P, N_TILES, K], BF16)
        xn = keep.tile([P, N_TILES, K], BF16)
        gained = keep.tile([P, P, PACK], F32)
        grouped = keep.tile([P, N_TILES, P, PACK], BF16, align_bytes=64)
        gain = keep.tile([P, PACK], BF16)
        bias = keep.tile([P, HEAD], BF16)
        bias_sides = keep.tile([P, 8], F32)
        bias_row = keep.tile([P, FEATURES], BF16)
        gain_row = keep.tile([P, K], BF16)
        ones = keep.tile([P, P], BF16)
        w_codes = keep.tile([P, FEATURES], U32, align_bytes=64)
        w_scales = keep.tile([P, BANK], U8, align_bytes=64)
        xq_codes = keep.tile([P, N_TILES, P], U32, align_bytes=64)
        xq_scales = keep.tile([P, N_TILES, P], U8, align_bytes=64)
        identity = keep.tile([P, P], F32)
        eps_rms = keep.tile([P, 1], F32)
        table_warm = keep.tile([P, 1], F32)
        sum_sq = keep.tile([P, N_TILES], F32)
        rstd = keep.tile([P, N_TILES], F32)
        right_sq = keep.tile([P, N_TILES], F32)
        right_floored = keep.tile([P, N_TILES], F32)
        right_inv = keep.tile([P, N_TILES], F32)
        floor = keep.tile([P, 1], F32)
        neg_floor = keep.tile([P, 1], F32)

        nc.vector.memset(eps_rms[:], EPS_RMS)
        nc.vector.memset(ones[:], 1.0)
        nc.vector.memset(gain_row[:].bitcast(I32), 0)
        nc.vector.memset(bias_row[:, 0:LEFT].bitcast(I32), 0)
        nc.vector.memset(w_scales[:].bitcast(I32), 0)
        nc.vector.memset(floor[:], EPS_NORM * EPS_NORM)
        nc.vector.memset(neg_floor[:], -EPS_NORM * EPS_NORM)
        nc.scalar.activation(out=table_warm[:], in_=eps_rms[:], func=ACT.Abs_reciprocal_sqrt)
        make_identity(nc, identity[:])
        nc.gpsimd.memset(bias_row[:, LEFT:].bitcast(F32), 0.0)


        def load_x(piece):
            first, end = piece
            nc.sync.dma_start(out=x_sb[:, first:end, :], in_=x_rows[:, first:end, :])

        def load_w(first, end):
            nc.sync.dma_start(
                out=w_codes[:, first:end].bitcast(I32),
                in_=w_bytes[:, PACK * first : PACK * end].bitcast(I32),
            )

        load_x(X_PIECES[0])
        nc.sync.dma_start(out=gain[:], in_=g.rearrange("(q t) -> q t", t=PACK))
        nc.sync.dma_start(out=gain_row[0:1, :], in_=g.unsqueeze(0))
        load_x(X_PIECES[1])
        nc.sync.dma_start(out=bias_row[0:1, 0:LEFT], in_=b1.unsqueeze(0)[:, 0:LEFT])
        nc.sync.dma_start(out=bias_row[0:1, LEFT:], in_=b1.unsqueeze(0)[:, LEFT:])
        load_x(X_PIECES[2])
        for quadrant in range(4):
            nc.sync.dma_start(
                out=w_scales[32 * quadrant : 32 * quadrant + 16, :].bitcast(I32),
                in_=w_scale_rows[4 * quadrant : 4 * quadrant + 4, :]
                .rearrange("r (j n) -> j r n", n=BANK)
                .bitcast(I32),
            )
        load_w(0, BANK)
        load_x(X_PIECES[3])
        load_w(BANK, HEAD)
        load_x(X_PIECES[4])
        load_w(RIGHT, FEATURES)
        load_w(LEFT, RIGHT)
        load_x(X_PIECES[5])


        def sum_squares(i):
            squares = work.tile([P, K], BF16)
            nc.scalar.activation(
                out=squares[:], in_=x_sb[:, i, :], func=ACT.Square, accum_out=sum_sq[:, i : i + 1]
            )

        def sum_squares_on_vector(i):
            squares = work.tile([P, K], BF16)
            nc.vector.scalar_tensor_tensor(
                out=squares[:],
                in0=x_sb[:, i, :],
                scalar=1.0,
                in1=x_sb[:, i, :],
                op0=ALU.mult,
                op1=ALU.mult,
                accum_out=sum_sq[:, i : i + 1],
            )

        def reciprocal_rms(first, end):
            nc.scalar.activation(
                out=rstd[:, first:end],
                in_=sum_sq[:, first:end],
                func=ACT.Abs_reciprocal_sqrt,
                scale=1.0 / K,
                bias=eps_rms[:],
            )

        def normalise_rows(i):
            nc.vector.scalar_tensor_tensor(
                out=xn[:, i, :],
                in0=x_sb[:, i, :],
                scalar=rstd[:, i : i + 1],
                in1=gain_spread[:],
                op0=ALU.mult,
                op1=ALU.mult,
            )

        flipped = {}

        def flip(rows, i):
            flipped[i] = flip_banks.tile([P, 2, P], F32, name="flipped")
            words = rows[:, i, :].bitcast(F32)
            for u in range(2):
                nc.tensor.transpose(flipped[i][:, u, :], words[:, u::2], identity[:])

        def group(copy, i):
            copy(
                out=grouped[:, i, :, :].bitcast(F32),
                in_=flipped[i][:].rearrange("q u r -> q r u"),
            )

        def quantise(i):
            nc.vector.quantize_mx(
                out=xq_codes[:, i, :].bitcast(FP8X4),
                scales=xq_scales[:, i, :],
                in_=grouped[:, i, :, :].rearrange("q r t -> q (r t)"),
            )

        right = {}
        wide = {}
        left = {}
        acc = {}

        def product(i, start):
            cols = slice(start, start + BANK)
            acc[(i, start)] = acc_banks.tile([P, BANK], F32, name="acc")
            nc.tensor.matmul_mx(
                out=acc[(i, start)][:],
                lhsT=xq_codes[:, i, :].bitcast(FP8X4),
                lhsT_scale=xq_scales[:, i, :],
                rhs=w_codes[:, cols].bitcast(FP8X4),
                rhs_scale=w_scales[PACK * (start // BANK) :, :],
                start=True,
                stop=True,
            )

        def add_bias(i, start):
            target = wide[i][:, start : start + BANK]
            nc.vector.tensor_tensor(
                out=target, in0=acc[(i, start)][:], in1=bias[:, start : start + BANK], op=ALU.add
            )

        def product_plus_bias(i, start):
            product(i, start)
            add_bias(i, start)

        clipped = {}
        back = {}

        def side_product(i, side):
            acc[(i, side)] = acc_banks.tile([P, 4, P], F32, name="acc")
            for c in range(4):
                cols = slice(side + c * P, side + (c + 1) * P)
                nc.tensor.matmul_mx(
                    out=acc[(i, side)][:, c, :],
                    lhsT=w_codes[:, cols].bitcast(FP8X4),
                    lhsT_scale=w_scales[PACK * (side // BANK) :, c * P : (c + 1) * P],
                    rhs=xq_codes[:, i, :].bitcast(FP8X4),
                    rhs_scale=xq_scales[:, i, :],
                    start=True,
                    stop=True,
                )

        def side_bias_relu(i, side):
            clipped[(i, side)] = clipped_tiles.tile([P, 4, P], F32, name="clipped_side")
            for c in (3, 2, 1, 0):
                column = (side - LEFT) // P + c
                nc.vector.tensor_scalar(
                    out=clipped[(i, side)][:, c, :],
                    in0=acc[(i, side)][:, c, :],
                    scalar1=bias_sides[:, column : column + 1],
                    scalar2=0.0,
                    op0=ALU.add,
                    op1=ALU.max,
                )

        def side_back(i, side):
            back[(i, side)] = back_bank.tile([P, 4, P], F32, name="back")
            for c in range(4):
                nc.tensor.transpose(back[(i, side)][:, c, :], clipped[(i, side)][:, c, :], identity[:])

        def side_square(i, side):
            target = right if side == RIGHT else left
            target[i] = results.tile([P, HALF], F32, name="side_results")
            nc.scalar.activation(
                out=target[i][:], in_=back[(i, side)][:].rearrange("p c f -> p (c f)"), func=ACT.Square
            )

        def store_left(i):
            nc.sync.dma_start(out=left_rows[:, i, :], in_=left[i][:])

        def relu(view):
            nc.gpsimd.tensor_scalar(
                out=view, in0=view, scalar1=FLT_BIG, scalar2=0.0, op0=ALU.min, op1=ALU.max
            )

        def square(view):
            nc.scalar.activation(out=view, in_=view, func=ACT.Square)

        def squared_relu(view):
            nc.vector.scalar_tensor_tensor(
                out=view, in0=view, scalar=0.0, in1=view, op0=ALU.max, op1=ALU.mult
            )

        def store_head(i, first, end):
            nc.sync.dma_start(out=head_rows[:, i, first:end], in_=wide[i][:, first:end])

        def sum_fourth(i):
            fourth = work.tile([P, HALF], F32)
            nc.scalar.activation(
                out=fourth[:], in_=right[i][:], func=ACT.Square, accum_out=right_sq[:, i : i + 1]
            )

        def floor_sum(i):
            nc.scalar.activation(
                out=right_floored[:, i : i + 1], in_=right_sq[:, i : i + 1], func=ACT.Relu, bias=neg_floor[:]
            )

        def reciprocal_norm(i):
            nc.scalar.activation(
                out=right_inv[:, i : i + 1],
                in_=right_floored[:, i : i + 1],
                func=ACT.Abs_reciprocal_sqrt,
                bias=floor[:],
            )

        def normalise_right_on_gpsimd(i):
            nc.gpsimd.tensor_scalar(
                out=right[i][:],
                in0=right[i][:],
                scalar1=right_inv[:, i : i + 1],
                scalar2=1.0,
                op0=ALU.mult,
                op1=ALU.mult,
            )

        def normalise_right(i):
            nc.vector.tensor_scalar_mul(out=right[i][:], in0=right[i][:], scalar1=right_inv[:, i : i + 1])

        def store_right(i):
            nc.sync.dma_start(out=right_rows[:, i, :], in_=right[i][:])

        spread = {}

        def spread_bias(first, end):
            spread[first] = acc_banks.tile([P, end - first], BF16, name="acc")
            for start in range(first, end, BANK):
                nc.tensor.matmul(
                    out=spread[first][:, start - first : start - first + BANK],
                    lhsT=ones[:],
                    rhs=bias_row[:, start : start + BANK],
                    start=True,
                    stop=True,
                )

        warm_up = acc_banks.tile([P, P], F32, name="acc")
        for repeat in range(WARM_UP):
            nc.tensor.matmul(out=warm_up[:], lhsT=ones[:], rhs=ones[:], start=True, stop=True)
        flip(x_sb, 0)
        nc.vector.tensor_tensor(
            out=gained[:].rearrange("q r (u e) -> q r u e", u=2),
            in0=flipped[0][:].rearrange("q u r -> q (u r)").bitcast(BF16).rearrange("q (u r e) -> q r u e", u=2, e=2),
            in1=gain[:].rearrange("q (u e) -> q u e", u=2).unsqueeze(1).to_broadcast([P, P, 2, 2]),
            op=ALU.mult,
        )
        sum_squares(0)
        reciprocal_rms(0, 1)
        gain_spread = gain_bank.tile([P, K], F32, name="gain_spread")
        nc.tensor.matmul(out=gain_spread[:], lhsT=ones[:], rhs=gain_row[:], start=True, stop=True)
        rstd_spread = acc_banks.tile([P, P], F32, name="acc")
        nc.tensor.matmul(
            out=rstd_spread[:], lhsT=rstd[:, 0:1].to_broadcast([P, P]), rhs=identity[:], start=True, stop=True
        )
        spread_bias(0, LEFT)
        sides_turned = acc_banks.tile([P, 8], F32, name="acc")
        for c in range(8):
            nc.tensor.matmul(
                out=sides_turned[:, c : c + 1],
                lhsT=bias_row[:, LEFT + c * P : LEFT + (c + 1) * P],
                rhs=ones[:, 0:1],
                start=True,
                stop=True,
            )
        sum_squares_on_vector(1)
        nc.vector.tensor_tensor(
            out=grouped[:, 0, :, :],
            in0=gained[:],
            in1=rstd_spread[:].unsqueeze(2).to_broadcast([P, P, PACK]),
            op=ALU.mult,
        )
        sum_squares(2)
        reciprocal_rms(1, 3)
        nc.scalar.copy(out=bias[:, 0:BANK], in_=spread[0][:, 0:BANK])
        nc.scalar.copy(out=bias[:, BANK:HEAD], in_=spread[0][:, BANK:HEAD])
        sum_squares(3)
        sum_squares(4)
        reciprocal_rms(3, 5)
        sum_squares(5)
        sum_squares(6)
        sum_squares(7)
        reciprocal_rms(5, 8)
        quantise(0)
        normalise_rows(1)
        nc.vector.tensor_copy(out=bias_sides[:], in_=sides_turned[:])

        wide[0] = heads_pool.tile([P, HEAD], F32, name="pre_wide")
        product(0, 0)
        flip(xn, 1)
        product(0, BANK)
        add_bias(0, 0)
        group(nc.vector.tensor_copy, 1)
        add_bias(0, BANK)
        relu(wide[0][:])
        quantise(1)
        side_product(0, RIGHT)
        side_product(0, LEFT)
        product(1, 0)
        product(1, BANK)
        normalise_rows(2)
        flip(xn, 2)
        side_bias_relu(0, RIGHT)
        side_back(0, RIGHT)
        side_bias_relu(0, LEFT)
        group(nc.vector.tensor_copy, 2)
        side_back(0, LEFT)
        square(wide[0][:])
        store_head(0, 0, HEAD)
        side_square(0, RIGHT)
        side_square(0, LEFT)
        store_left(0)
        sum_fourth(0)

        for i in range(1, N_TILES):
            wide[i] = heads_pool.tile([P, HEAD], F32, name="pre_wide")
            if i < LAST:
                add_bias(i, 0)
                add_bias(i, BANK)
                quantise(i + 1)
                side_product(i, RIGHT)
                side_product(i, LEFT)
            if i < LAST - 1:
                relu(wide[i][:])
                if i > 1:
                    normalise_right_on_gpsimd(i - 2)
            if i < LAST - 1:
                product(i + 1, 0)
                product(i + 1, BANK)
            elif i == LAST - 1:
                side_product(LAST, RIGHT)
                side_product(LAST, LEFT)
            else:
                product(i, 0)
                product(i, BANK)
            if i + 2 < N_TILES:
                normalise_rows(i + 2)
                flip(xn, i + 2)
            side_bias_relu(i, RIGHT)
            side_back(i, RIGHT)
            side_bias_relu(i, LEFT)
            if i + 2 < N_TILES:
                group(nc.scalar.copy if i + 2 in (4, 5, 6) else nc.vector.tensor_copy, i + 2)
            side_back(i, LEFT)
            if i < LAST - 1:
                if i > 1:
                    store_right(i - 2)
                square(wide[i][:])
                store_head(i, 0, HEAD)
                floor_sum(i - 1)
                side_square(i, RIGHT)
                reciprocal_norm(i - 1)
                side_square(i, LEFT)
                store_left(i)
                sum_fourth(i)
            elif i == LAST - 1:
                floor_sum(i - 1)
                side_square(i, RIGHT)
                reciprocal_norm(i - 1)
                side_square(i, LEFT)
                normalise_right(i - 2)
                store_right(i - 2)
                store_left(i)
                sum_fourth(i)
            else:
                squared_relu(wide[i - 1][:, 0:BANK])
                store_head(i - 1, 0, BANK)
                normalise_right(i - 2)
                store_right(i - 2)
                squared_relu(wide[i - 1][:, BANK:HEAD])
                store_head(i - 1, BANK, HEAD)
                add_bias(i, 0)
                add_bias(i, BANK)
                side_square(i, RIGHT)
                floor_sum(i - 1)
                side_square(i, LEFT)
                reciprocal_norm(i - 1)
                sum_fourth(i)
                store_left(i)
                squared_relu(wide[i][:, 0:BANK])
                store_head(i, 0, BANK)
                normalise_right(i - 1)
                store_right(i - 1)
                squared_relu(wide[i][:, BANK:HEAD])
                store_head(i, BANK, HEAD)
                floor_sum(i)
                reciprocal_norm(i)
                normalise_right(i)
                store_right(i)
